import numpy as np
import ml_dtypes


def mxq(x, axis, fmt="e4m3"):
    dtype, down = {"e4m3": (ml_dtypes.float8_e4m3fn, 7), "e5m2": (ml_dtypes.float8_e5m2, 14)}[fmt]
    v = np.moveaxis(np.asarray(x, np.float32).astype(ml_dtypes.bfloat16).astype(np.float64), axis, -1)
    blocks = v.reshape(v.shape[:-1] + (-1, 32))
    amax = np.abs(blocks).max(-1, keepdims=True)
    byte = np.maximum(np.where(amax > 0, np.frexp(amax)[1] - 1 + 127, 0) - down, 1)
    scale = np.exp2(byte - 127.0)
    codes = (blocks / scale).astype(np.float32).astype(dtype).astype(np.float64)
    return np.moveaxis((codes * scale).reshape(v.shape), -1, axis)


WIDE = False


def mx_kscale(k):
    if not WIDE:
        return np.ones(k)
    levels = np.array([10, -10, 5, -5, 0])
    a = np.random.permutation(np.resize(levels, k // 512 * 4)).reshape(k // 512, 4)
    idx = np.arange(k)
    return np.exp2(a[idx // 512, idx % 128 // 32])


BF16 = ml_dtypes.bfloat16


def bf(x):
    return np.asarray(x, np.float32).astype(BF16)


def f64(x):
    return np.asarray(x).astype(np.float64)


E2M1 = np.array([0.0, 0.5, 1.0, 1.5, 2.0, 3.0, 4.0, 6.0, -0.0, -0.5, -1.0, -1.5, -2.0, -3.0, -4.0, -6.0])


def pack_weight(w, fmt):
    k, n = w.shape
    w = f64(bf(w)).reshape(k // 32, 32, n)
    amax = np.abs(w).max(1)
    if fmt == "e4m3":
        byte = np.frexp(amax)[1] - 1 + 127 - 7
    else:
        mant, ex = np.frexp(amax / 6.0)
        byte = np.where(mant > 0.5, ex, ex - 1) + 127
    byte = np.clip(np.where(amax > 0, byte, 1), 1, 254)
    scaled = (w * np.exp2(127.0 - byte)[:, None, :]).reshape(k, n).astype(np.float32)
    by_word = np.ascontiguousarray(scaled.reshape(k // 512, 128, 4, n).transpose(0, 1, 3, 2))
    if fmt == "e4m3":
        words = by_word.astype(ml_dtypes.float8_e4m3fn).view(np.uint8)
    else:
        c = by_word.astype(ml_dtypes.float4_e2m1fn).view(np.uint8) & 0xF
        words = c[..., 0::2] | (c[..., 1::2] << 4)
    return np.ascontiguousarray(words), np.ascontiguousarray(byte.astype(np.uint8).reshape(k // 512, 16, n))


def unpack_weight(words, scales, fmt):
    g, p, n, _ = words.shape
    if fmt == "e4m3":
        vals = np.ascontiguousarray(words).view(ml_dtypes.float8_e4m3fn).astype(np.float64)
    else:
        nib = np.empty((g, p, n, 4), np.uint8)
        nib[..., 0::2] = words & 0xF
        nib[..., 1::2] = words >> 4
        vals = E2M1[nib]
    vals = vals * np.repeat(np.exp2(scales.astype(np.float64) - 127.0), 8, axis=1)[..., None]
    return vals.transpose(0, 1, 3, 2).reshape(g * 512, n)

def pack4(w):
    words, scales = pack_weight(w, "e2m1")
    return words.reshape(words.shape[0], 128, -1), scales


def unpack4(words, scales):
    return unpack_weight(words.reshape(words.shape[0], 128, -1, 2), scales, "e2m1")


N, C, F, G = 256, 3, 256, 16384
F2 = F + F
F3 = F2 + F


def silu(v):
    return v / (1.0 + np.exp(-v))


def setup_inputs():
    s = mx_kscale(G)
    h = bf(silu(1.4 * np.random.standard_normal((N, 1, G))) * s)
    mu_W = bf(np.random.standard_normal((N, C, F)))
    mu_VW = bf(np.sqrt(C) * np.random.standard_normal((N, 1, F)))
    q = bf(np.random.standard_normal((N, 1, F)))
    mu = bf(np.random.standard_normal((N, C, F)))
    W2 = np.random.standard_normal((F3, G)) / np.sqrt(G) / s
    words, scales = pack4(np.ascontiguousarray(W2.T))
    b2 = bf(0.2 * np.random.standard_normal(F3))
    return {"h": h,
            "mu_W": mu_W,
            "mu_VW": mu_VW,
            "q": q,
            "mu": mu,
            "W2_words": words,
            "W2_scales": scales,
            "b2": b2}


def reference(h, mu_W, mu_VW, q, mu, W2_words, W2_scales, b2):
    x = (mxq(f64(h), 2, "e4m3") @ unpack4(W2_words, W2_scales)) + f64(b2)
    dq_intra = x[..., :F]
    dmu_intra = x[..., F:F2] * f64(mu_W)
    dqmu_intra = x[..., F2:] * f64(mu_VW)
    q_out = f64(q) + dq_intra + dqmu_intra
    mu_out = f64(mu) + dmu_intra
    return q_out, mu_out

@@ -1,0 +1,228 @@
+import concourse.mybir as mybir
+from concourse.masks import make_identity
+
+F32 = mybir.dt.float32
+BF16 = mybir.dt.bfloat16
+I32 = mybir.dt.int32
+U32 = mybir.dt.uint32
+U8 = mybir.dt.uint8
+FP8X4 = mybir.dt.float8_e4m3fn_x4
+FP4X4 = mybir.dt.float4_e2m1fn_x4
+MULT = mybir.AluOpType.mult
+ADD = mybir.AluOpType.add
+
+P = 128
+ATOMS = 256
+ATOM_TILES = ATOMS // P
+K = 16384
+PACK = 4
+K_PASS = P * PACK
+PASSES = K // K_PASS
+PAIRS = PACK // 2
+F = 256
+AXES = 3
+COLS = 3 * F
+
+WIDE = (0, 512)
+NARROW = ((512, 128), (640, 128))
+
+QUANT_PASSES = 4
+SCALE_PASSES = 8
+WORD_PASSES = 4
+LAST_RUN = 8
+
+FLOPS = 2 * ATOMS * K * COLS
+
+
+def tile_painnmixing_pb_k_kernel(
+    tc, h, mu_W, mu_VW, q, mu, W2_words, W2_scales, b2, out_0, out_1
+):
+    nc = tc.nc
+    with (
+        tc.tile_pool(name="keep", bufs=1) as keep,
+        tc.tile_pool(name="stage", bufs=2) as stage,
+        tc.psum_pool(name="bias_banks", bufs=1) as bias_banks,
+        tc.psum_pool(name="banks", bufs=6) as banks,
+    ):
+        h_sb = keep.tile([P, ATOM_TILES, K], BF16)
+        h_codes = keep.tile([P, PASSES, ATOMS], U32, align_bytes=64)
+        h_scales = keep.tile([P, PASSES, ATOMS], U8, align_bytes=64)
+        w_words = keep.tile([P, PASSES, 2 * COLS], U8, align_bytes=64)
+        w_scales = keep.tile([P, PASSES, COLS], U8, align_bytes=64)
+        identity = keep.tile([P, P], F32)
+        ones = keep.tile([P, P], BF16)
+        bias_rows = keep.tile([P, COLS], BF16)
+        mu_w_sb = keep.tile([P, ATOM_TILES, AXES, F], BF16)
+        mu_sb = keep.tile([P, ATOM_TILES, AXES, F], BF16)
+        mu_vw_sb = keep.tile([P, ATOM_TILES, F], BF16)
+        q_sb = keep.tile([P, ATOM_TILES, F], BF16)
+        base_mu = keep.tile([P, ATOM_TILES, AXES, F], F32)
+        base_q = keep.tile([P, ATOM_TILES, F], F32)
+        mu_new = keep.tile([P, ATOM_TILES, AXES, F], F32)
+        q_new = keep.tile([P, ATOM_TILES, F], F32)
+        gate = keep.tile([P, ATOM_TILES, F], F32)
+
+        nc.vector.memset(bias_rows[:], 0.0)
+        nc.vector.memset(ones[:], 1.0)
+        nc.vector.memset(w_scales[:].bitcast(I32), 0)
+        make_identity(nc, identity[:])
+
+        nc.scalar.dma_start(out=bias_rows[0:1, :], in_=b2.unsqueeze(0))
+
+        h_rows = h.rearrange("n o k -> n (o k)")
+        k_load = QUANT_PASSES * K_PASS
+        for unit in range(PASSES // QUANT_PASSES):
+            ks = slice(unit * k_load, (unit + 1) * k_load)
+            for m in range(ATOM_TILES):
+                nc.sync.dma_start(out=h_sb[:, m, ks], in_=h_rows[m * P : (m + 1) * P, ks])
+
+        def load_small_inputs():
+            nc.sync.dma_start(
+                out=mu_w_sb[:], in_=mu_W.rearrange("(m p) c f -> p m c f", p=P)
+            )
+            nc.sync.dma_start(out=mu_sb[:], in_=mu.rearrange("(m p) c f -> p m c f", p=P))
+            nc.sync.dma_start(
+                out=mu_vw_sb[:], in_=mu_VW.rearrange("(m p) o f -> p m (o f)", p=P)
+            )
+            nc.sync.dma_start(out=q_sb[:], in_=q.rearrange("(m p) o f -> p m (o f)", p=P))
+
+        w_words_i32 = w_words[:].bitcast(I32)
+        w_scales_i32 = w_scales[:].bitcast(I32)
+        words_dram = W2_words.bitcast(I32)
+        scales_dram = W2_scales.bitcast(I32)
+        for run in range(PASSES // SCALE_PASSES):
+            gs = slice(run * SCALE_PASSES, (run + 1) * SCALE_PASSES)
+            for b in range(2):
+                for r in range(4):
+                    nc.sync.dma_start(
+                        out=w_scales_i32[32 * b + r : P : 64, gs, :],
+                        in_=scales_dram[gs, 4 * b + r : 16 : 8, :].rearrange("g s n -> s g n"),
+                    )
+            for part in range(SCALE_PASSES // WORD_PASSES):
+                g0 = run * SCALE_PASSES + part * WORD_PASSES
+                nc.sync.dma_start(
+                    out=w_words_i32[:, g0 : g0 + WORD_PASSES, :],
+                    in_=words_dram[g0 : g0 + WORD_PASSES].rearrange("g p n -> p g n"),
+                )
+            if run == 1:
+                load_small_inputs()
+
+        bias_wide = bias_banks.tile([P, WIDE[1]], F32)
+        bias_narrow = bias_banks.tile([P, COLS - WIDE[1]], F32)
+        nc.tensor.matmul(
+            out=bias_wide[:], lhsT=ones[:], rhs=bias_rows[:, : WIDE[1]], start=True, stop=True
+        )
+        nc.tensor.matmul(
+            out=bias_narrow[:], lhsT=ones[:], rhs=bias_rows[:, WIDE[1] :], start=True, stop=True
+        )
+
+        h_words = h_sb[:].bitcast(F32)
+        words_pass = K_PASS // 2
+        for unit in range(PASSES // QUANT_PASSES):
+            grouped = stage.tile([P, QUANT_PASSES, ATOMS, PACK], BF16, align_bytes=64)
+            grouped_words = grouped[:].bitcast(F32)
+            for j in range(QUANT_PASSES):
+                g = unit * QUANT_PASSES + j
+                flipped = banks.tile([P, PAIRS, ATOMS], F32, tag="bank")
+                for u in range(PAIRS):
+                    for m in range(ATOM_TILES):
+                        nc.tensor.transpose(
+                            flipped[:, u, m * P : (m + 1) * P],
+                            h_words[:, m, words_pass * g + u : words_pass * (g + 1) : PAIRS],
+                            identity[:],
+                        )
+                together = flipped[:].rearrange("p u a -> p a u")
+                if j == QUANT_PASSES - 1:
+                    nc.vector.tensor_copy(out=grouped_words[:, j], in_=together)
+                else:
+                    nc.scalar.copy(out=grouped_words[:, j], in_=together)
+            gs = slice(unit * QUANT_PASSES, (unit + 1) * QUANT_PASSES)
+            nc.vector.quantize_mx(
+                out=h_codes[:, gs, :].rearrange("p g a -> p (g a)").bitcast(FP8X4),
+                scales=h_scales[:, gs, :].rearrange("p g a -> p (g a)"),
+                in_=grouped[:].rearrange("p g a t -> p (g a t)"),
+            )
+
+        nc.vector.tensor_tensor(
+            out=base_mu[:].rearrange("p m c f -> p (m c) f"),
+            in0=mu_w_sb[:].rearrange("p m c f -> p (m c) f"),
+            in1=bias_wide[:, F : 2 * F].unsqueeze(1).to_broadcast([P, ATOM_TILES * AXES, F]),
+            op=MULT,
+        )
+        nc.vector.tensor_tensor(out=base_mu[:], in0=base_mu[:], in1=mu_sb[:], op=ADD)
+        nc.vector.tensor_tensor(
+            out=base_q[:],
+            in0=mu_vw_sb[:],
+            in1=bias_narrow[:].unsqueeze(1).to_broadcast([P, ATOM_TILES, F]),
+            op=MULT,
+        )
+        nc.vector.tensor_tensor(
+            out=base_q[:],
+            in0=base_q[:],
+            in1=bias_wide[:, :F].unsqueeze(1).to_broadcast([P, ATOM_TILES, F]),
+            op=ADD,
+        )
+        nc.vector.tensor_tensor(out=base_q[:], in0=base_q[:], in1=q_sb[:], op=ADD)
+
+        sums = {}
+        for m in range(ATOM_TILES):
+            for block in (WIDE,) + NARROW:
+                sums[(m, block)] = banks.tile(
+                    [P, block[1]], F32, tag="bank", name="sum_%d_%d" % (m, block[0])
+                )
+
+        def mx_pass(g, m, block):
+            first, width = block
+            atoms = slice(m * P, (m + 1) * P)
+            nc.tensor.matmul_mx(
+                out=sums[(m, block)][:],
+                lhsT=h_codes[:, g, atoms].bitcast(FP8X4),
+                lhsT_scale=h_scales[:, g, atoms],
+                rhs=w_words[:, g, 2 * first : 2 * (first + width)].bitcast(FP4X4),
+                rhs_scale=w_scales[:, g, first : first + width],
+                start=(g == 0),
+                stop=(g == PASSES - 1),
+            )
+
+        for g in range(PASSES - LAST_RUN):
+            for m in range(ATOM_TILES):
+                for block in (WIDE,) + NARROW:
+                    mx_pass(g, m, block)
+        last_passes = range(PASSES - LAST_RUN, PASSES)
+        for m in range(ATOM_TILES):
+            for g in last_passes:
+                mx_pass(g, m, WIDE)
+        for m in range(ATOM_TILES):
+            for block in NARROW:
+                for g in last_passes:
+                    mx_pass(g, m, block)
+
+        for m in range(ATOM_TILES):
+            wide = sums[(m, WIDE)]
+            nc.vector.tensor_tensor(
+                out=mu_new[:, m],
+                in0=mu_w_sb[:, m],
+                in1=wide[:, F : 2 * F].unsqueeze(1).to_broadcast([P, AXES, F]),
+                op=MULT,
+            )
+            nc.vector.tensor_tensor(out=q_new[:, m], in0=base_q[:, m], in1=wide[:, :F], op=ADD)
+            nc.vector.tensor_tensor(
+                out=mu_new[:, m], in0=mu_new[:, m], in1=base_mu[:, m], op=ADD
+            )
+            nc.sync.dma_start(
+                out=out_1[m * P : (m + 1) * P].rearrange("n c f -> n (c f)"),
+                in_=mu_new[:, m].rearrange("p c f -> p (c f)"),
+            )
+        for m in range(ATOM_TILES):
+            for block in NARROW:
+                cols = slice(block[0] - 2 * F, block[0] - 2 * F + block[1])
+                nc.vector.tensor_tensor(
+                    out=gate[:, m, cols],
+                    in0=mu_vw_sb[:, m, cols],
+                    in1=sums[(m, block)][:],
+                    op=MULT,
+                )
+            nc.vector.tensor_tensor(out=q_new[:, m], in0=q_new[:, m], in1=gate[:, m], op=ADD)
+            nc.sync.dma_start(
+                out=out_0[m * P : (m + 1) * P].rearrange("n o f -> n (o f)"), in_=q_new[:, m]
+            )

@@ -28,7 +28,7 @@ NARROW = ((512, 128), (640, 128))
 
 QUANT_PASSES = 4
 SCALE_PASSES = 8
-WORD_PASSES = 4
+WORD_PASSES = 2
 LAST_RUN = 8
 
 FLOPS = 2 * ATOMS * K * COLS
@@ -43,6 +43,7 @@ def tile_painnmixing_pb_k_kernel(
         tc.tile_pool(name="stage", bufs=2) as stage,
         tc.psum_pool(name="bias_banks", bufs=1) as bias_banks,
         tc.psum_pool(name="banks", bufs=6) as banks,
+        tc.manual_schedule(),
     ):
         h_sb = keep.tile([P, ATOM_TILES, K], BF16)
         h_codes = keep.tile([P, PASSES, ATOMS], U32, align_bytes=64)
@@ -107,15 +108,6 @@ def tile_painnmixing_pb_k_kernel(
             if run == 1:
                 load_small_inputs()
 
-        bias_wide = bias_banks.tile([P, WIDE[1]], F32)
-        bias_narrow = bias_banks.tile([P, COLS - WIDE[1]], F32)
-        nc.tensor.matmul(
-            out=bias_wide[:], lhsT=ones[:], rhs=bias_rows[:, : WIDE[1]], start=True, stop=True
-        )
-        nc.tensor.matmul(
-            out=bias_narrow[:], lhsT=ones[:], rhs=bias_rows[:, WIDE[1] :], start=True, stop=True
-        )
-
         h_words = h_sb[:].bitcast(F32)
         words_pass = K_PASS // 2
         for unit in range(PASSES // QUANT_PASSES):
@@ -142,6 +134,15 @@ def tile_painnmixing_pb_k_kernel(
                 scales=h_scales[:, gs, :].rearrange("p g a -> p (g a)"),
                 in_=grouped[:].rearrange("p g a t -> p (g a t)"),
             )
+
+        bias_wide = bias_banks.tile([P, WIDE[1]], F32)
+        bias_narrow = bias_banks.tile([P, COLS - WIDE[1]], F32)
+        nc.tensor.matmul(
+            out=bias_wide[:], lhsT=ones[:], rhs=bias_rows[:, : WIDE[1]], start=True, stop=True
+        )
+        nc.tensor.matmul(
+            out=bias_narrow[:], lhsT=ones[:], rhs=bias_rows[:, WIDE[1] :], start=True, stop=True
+        )
 
         nc.vector.tensor_tensor(
             out=base_mu[:].rearrange("p m c f -> p (m c) f"),

@@ -48,8 +48,14 @@ def tile_painnmixing_pb_k_kernel(
         h_sb = keep.tile([P, ATOM_TILES, K], BF16)
         h_codes = keep.tile([P, PASSES, ATOMS], U32, align_bytes=64)
         h_scales = keep.tile([P, PASSES, ATOMS], U8, align_bytes=64)
-        w_words = keep.tile([P, PASSES, 2 * COLS], U8, align_bytes=64)
-        w_scales = keep.tile([P, PASSES, COLS], U8, align_bytes=64)
+        w_words = [
+            keep.tile([P, WORD_PASSES, 2 * COLS], U8, align_bytes=64, name="w_words_%d" % i)
+            for i in range(PASSES // WORD_PASSES)
+        ]
+        w_scales = [
+            keep.tile([P, SCALE_PASSES, COLS], U8, align_bytes=64, name="w_scales_%d" % i)
+            for i in range(PASSES // SCALE_PASSES)
+        ]
         identity = keep.tile([P, P], F32)
         ones = keep.tile([P, P], BF16)
         bias_rows = keep.tile([P, COLS], BF16)
@@ -65,7 +71,8 @@ def tile_painnmixing_pb_k_kernel(
 
         nc.vector.memset(bias_rows[:], 0.0)
         nc.vector.memset(ones[:], 1.0)
-        nc.vector.memset(w_scales[:].bitcast(I32), 0)
+        for plane in w_scales:
+            nc.vector.memset(plane[:].bitcast(I32), 0)
         make_identity(nc, identity[:])
 
         nc.scalar.dma_start(out=bias_rows[0:1, :], in_=b2.unsqueeze(0))
@@ -87,8 +94,6 @@ def tile_painnmixing_pb_k_kernel(
             )
             nc.sync.dma_start(out=q_sb[:], in_=q.rearrange("(m p) o f -> p m (o f)", p=P))
 
-        w_words_i32 = w_words[:].bitcast(I32)
-        w_scales_i32 = w_scales[:].bitcast(I32)
         words_dram = W2_words.bitcast(I32)
         scales_dram = W2_scales.bitcast(I32)
         for run in range(PASSES // SCALE_PASSES):
@@ -96,13 +101,13 @@ def tile_painnmixing_pb_k_kernel(
             for b in range(2):
                 for r in range(4):
                     nc.sync.dma_start(
-                        out=w_scales_i32[32 * b + r : P : 64, gs, :],
+                        out=w_scales[run][32 * b + r : P : 64].bitcast(I32),
                         in_=scales_dram[gs, 4 * b + r : 16 : 8, :].rearrange("g s n -> s g n"),
                     )
             for part in range(SCALE_PASSES // WORD_PASSES):
                 g0 = run * SCALE_PASSES + part * WORD_PASSES
                 nc.sync.dma_start(
-                    out=w_words_i32[:, g0 : g0 + WORD_PASSES, :],
+                    out=w_words[g0 // WORD_PASSES][:].bitcast(I32),
                     in_=words_dram[g0 : g0 + WORD_PASSES].rearrange("g p n -> p g n"),
                 )
             if run == 1:
@@ -179,8 +184,10 @@ def tile_painnmixing_pb_k_kernel(
                 out=sums[(m, block)][:],
                 lhsT=h_codes[:, g, atoms].bitcast(FP8X4),
                 lhsT_scale=h_scales[:, g, atoms],
-                rhs=w_words[:, g, 2 * first : 2 * (first + width)].bitcast(FP4X4),
-                rhs_scale=w_scales[:, g, first : first + width],
+                rhs=w_words[g // WORD_PASSES][
+                    :, g % WORD_PASSES, 2 * first : 2 * (first + width)
+                ].bitcast(FP4X4),
+                rhs_scale=w_scales[g // SCALE_PASSES][:, g % SCALE_PASSES, first : first + width],
                 start=(g == 0),
                 stop=(g == PASSES - 1),
             )

@@ -27,7 +27,7 @@ WIDE = (0, 512)
 NARROW = ((512, 128), (640, 128))
 
 QUANT_PASSES = 4
-SCALE_PASSES = 8
+SCALE_PASSES = 16
 WORD_PASSES = 2
 LAST_RUN = 8
 
@@ -94,23 +94,23 @@ def tile_painnmixing_pb_k_kernel(
             )
             nc.sync.dma_start(out=q_sb[:], in_=q.rearrange("(m p) o f -> p m (o f)", p=P))
 
-        words_dram = W2_words.bitcast(I32)
-        scales_dram = W2_scales.bitcast(I32)
+        scales_dram = W2_scales.bitcast(F32)
         for run in range(PASSES // SCALE_PASSES):
             gs = slice(run * SCALE_PASSES, (run + 1) * SCALE_PASSES)
             for b in range(2):
                 for r in range(4):
-                    nc.sync.dma_start(
-                        out=w_scales[run][32 * b + r : P : 64].bitcast(I32),
+                    nc.gpsimd.dma_start(
+                        out=w_scales[run][32 * b + r : P : 64].bitcast(F32),
                         in_=scales_dram[gs, 4 * b + r : 16 : 8, :].rearrange("g s n -> s g n"),
                     )
-            for part in range(SCALE_PASSES // WORD_PASSES):
-                g0 = run * SCALE_PASSES + part * WORD_PASSES
-                nc.sync.dma_start(
-                    out=w_words[g0 // WORD_PASSES][:].bitcast(I32),
-                    in_=words_dram[g0 : g0 + WORD_PASSES].rearrange("g p n -> p g n"),
-                )
-            if run == 1:
+
+        words_dram = W2_words.bitcast(I32)
+        for i in range(PASSES // WORD_PASSES):
+            nc.sync.dma_start(
+                out=w_words[i][:].bitcast(I32),
+                in_=words_dram[i * WORD_PASSES : (i + 1) * WORD_PASSES].rearrange("g p n -> p g n"),
+            )
+            if i == PASSES // WORD_PASSES // 2:
                 load_small_inputs()
 
         h_words = h_sb[:].bitcast(F32)

@@ -27,9 +27,11 @@ WIDE = (0, 512)
 NARROW = ((512, 128), (640, 128))
 
 QUANT_PASSES = 4
-SCALE_PASSES = 16
+SCALE_PASSES = 8
 WORD_PASSES = 2
 LAST_RUN = 8
+
+assert SCALE_PASSES // WORD_PASSES == 4
 
 FLOPS = 2 * ATOMS * K * COLS
 
@@ -77,41 +79,45 @@ def tile_painnmixing_pb_k_kernel(
 
         nc.scalar.dma_start(out=bias_rows[0:1, :], in_=b2.unsqueeze(0))
 
+        words_dram = W2_words.bitcast(I32)
+        scales_dram = W2_scales.bitcast(I32)
+
+        def load_scale_rows(run, quarter):
+            gs = slice(run * SCALE_PASSES, (run + 1) * SCALE_PASSES)
+            for b, r in (divmod(2 * quarter, 4), divmod(2 * quarter + 1, 4)):
+                nc.sync.dma_start(
+                    out=w_scales[run][32 * b + r : P : 64].bitcast(I32),
+                    in_=scales_dram[gs, 4 * b + r : 16 : 8, :].rearrange("g s n -> s g n"),
+                )
+
         h_rows = h.rearrange("n o k -> n (o k)")
         k_load = QUANT_PASSES * K_PASS
-        for unit in range(PASSES // QUANT_PASSES):
+        h_loads = ATOM_TILES * PASSES // QUANT_PASSES
+        for i in range(h_loads):
+            unit, m = divmod(i, ATOM_TILES)
             ks = slice(unit * k_load, (unit + 1) * k_load)
-            for m in range(ATOM_TILES):
-                nc.sync.dma_start(out=h_sb[:, m, ks], in_=h_rows[m * P : (m + 1) * P, ks])
+            nc.sync.dma_start(out=h_sb[:, m, ks], in_=h_rows[m * P : (m + 1) * P, ks])
+            if i >= h_loads - 4:
+                load_scale_rows(0, i - (h_loads - 4))
 
-        def load_small_inputs():
-            nc.sync.dma_start(
-                out=mu_w_sb[:], in_=mu_W.rearrange("(m p) c f -> p m c f", p=P)
-            )
-            nc.sync.dma_start(out=mu_sb[:], in_=mu.rearrange("(m p) c f -> p m c f", p=P))
-            nc.sync.dma_start(
-                out=mu_vw_sb[:], in_=mu_VW.rearrange("(m p) o f -> p m (o f)", p=P)
-            )
-            nc.sync.dma_start(out=q_sb[:], in_=q.rearrange("(m p) o f -> p m (o f)", p=P))
-
-        scales_dram = W2_scales.bitcast(F32)
-        for run in range(PASSES // SCALE_PASSES):
-            gs = slice(run * SCALE_PASSES, (run + 1) * SCALE_PASSES)
-            for b in range(2):
-                for r in range(4):
-                    nc.gpsimd.dma_start(
-                        out=w_scales[run][32 * b + r : P : 64].bitcast(F32),
-                        in_=scales_dram[gs, 4 * b + r : 16 : 8, :].rearrange("g s n -> s g n"),
-                    )
-
-        words_dram = W2_words.bitcast(I32)
+        loads_a_run = SCALE_PASSES // WORD_PASSES
         for i in range(PASSES // WORD_PASSES):
             nc.sync.dma_start(
                 out=w_words[i][:].bitcast(I32),
                 in_=words_dram[i * WORD_PASSES : (i + 1) * WORD_PASSES].rearrange("g p n -> p g n"),
             )
-            if i == PASSES // WORD_PASSES // 2:
-                load_small_inputs()
+            next_run = i // loads_a_run + 1
+            if next_run < PASSES // SCALE_PASSES:
+                load_scale_rows(next_run, i % loads_a_run)
+            if i == PASSES // WORD_PASSES // 2 - 1:
+                nc.sync.dma_start(
+                    out=mu_w_sb[:], in_=mu_W.rearrange("(m p) c f -> p m c f", p=P)
+                )
+                nc.sync.dma_start(out=mu_sb[:], in_=mu.rearrange("(m p) c f -> p m c f", p=P))
+                nc.sync.dma_start(
+                    out=mu_vw_sb[:], in_=mu_VW.rearrange("(m p) o f -> p m (o f)", p=P)
+                )
+                nc.sync.dma_start(out=q_sb[:], in_=q.rearrange("(m p) o f -> p m (o f)", p=P))
 
         h_words = h_sb[:].bitcast(F32)
         words_pass = K_PASS // 2

@@ -23,15 +23,12 @@ F = 256
 AXES = 3
 COLS = 3 * F
 
-WIDE = (0, 512)
-NARROW = ((512, 128), (640, 128))
+NARROW = 128
+WIDE = 512
 
-QUANT_PASSES = 4
+UNITS = [(0, 2), (2, 2)] + [(g, 4) for g in range(4, PASSES, 4)]
+TAIL_UNITS = (len(UNITS) - 2, len(UNITS) - 1)
 SCALE_PASSES = 8
-WORD_PASSES = 2
-LAST_RUN = 8
-
-assert SCALE_PASSES // WORD_PASSES == 4
 
 FLOPS = 2 * ATOMS * K * COLS
 
@@ -42,17 +39,17 @@ def tile_painnmixing_pb_k_kernel(
     nc = tc.nc
     with (
         tc.tile_pool(name="keep", bufs=1) as keep,
-        tc.tile_pool(name="stage", bufs=2) as stage,
-        tc.psum_pool(name="bias_banks", bufs=1) as bias_banks,
-        tc.psum_pool(name="banks", bufs=6) as banks,
+        tc.tile_pool(name="stage", bufs=3) as stage,
+        tc.psum_pool(name="sum_banks", bufs=1) as sum_banks,
+        tc.psum_pool(name="flip_banks", bufs=5) as flip_banks,
         tc.manual_schedule(),
     ):
-        h_sb = keep.tile([P, ATOM_TILES, K], BF16)
-        h_codes = keep.tile([P, PASSES, ATOMS], U32, align_bytes=64)
-        h_scales = keep.tile([P, PASSES, ATOMS], U8, align_bytes=64)
+        h_sb = [
+            keep.tile([P, ATOM_TILES, n * K_PASS], BF16, name="h_%d" % g) for g, n in UNITS
+        ]
         w_words = [
-            keep.tile([P, WORD_PASSES, 2 * COLS], U8, align_bytes=64, name="w_words_%d" % i)
-            for i in range(PASSES // WORD_PASSES)
+            keep.tile([P, n, 2 * COLS], U8, align_bytes=64, name="w_words_%d" % g)
+            for g, n in UNITS
         ]
         w_scales = [
             keep.tile([P, SCALE_PASSES, COLS], U8, align_bytes=64, name="w_scales_%d" % i)
@@ -61,182 +58,242 @@ def tile_painnmixing_pb_k_kernel(
         identity = keep.tile([P, P], F32)
         ones = keep.tile([P, P], BF16)
         bias_rows = keep.tile([P, COLS], BF16)
+        bias = keep.tile([P, COLS], F32)
         mu_w_sb = keep.tile([P, ATOM_TILES, AXES, F], BF16)
         mu_sb = keep.tile([P, ATOM_TILES, AXES, F], BF16)
         mu_vw_sb = keep.tile([P, ATOM_TILES, F], BF16)
         q_sb = keep.tile([P, ATOM_TILES, F], BF16)
         base_mu = keep.tile([P, ATOM_TILES, AXES, F], F32)
         base_q = keep.tile([P, ATOM_TILES, F], F32)
+        narrow_sum = keep.tile([P, ATOM_TILES, F], F32)
         mu_new = keep.tile([P, ATOM_TILES, AXES, F], F32)
         q_new = keep.tile([P, ATOM_TILES, F], F32)
         gate = keep.tile([P, ATOM_TILES, F], F32)
 
-        nc.vector.memset(bias_rows[:], 0.0)
-        nc.vector.memset(ones[:], 1.0)
-        for plane in w_scales:
-            nc.vector.memset(plane[:].bitcast(I32), 0)
+        nc.vector.memset(w_scales[0][:].bitcast(I32), 0)
         make_identity(nc, identity[:])
+        nc.gpsimd.memset(bias_rows[:], 0.0)
+        nc.gpsimd.memset(ones[:], 1.0)
+        for plane in w_scales[1:]:
+            nc.gpsimd.memset(plane[:].bitcast(I32), 0)
 
         nc.scalar.dma_start(out=bias_rows[0:1, :], in_=b2.unsqueeze(0))
 
         words_dram = W2_words.bitcast(I32)
         scales_dram = W2_scales.bitcast(I32)
+        h_rows = h.rearrange("(p m) o k -> p m (o k)", p=P)
 
-        def load_scale_rows(run, quarter):
-            gs = slice(run * SCALE_PASSES, (run + 1) * SCALE_PASSES)
-            for b, r in (divmod(2 * quarter, 4), divmod(2 * quarter + 1, 4)):
-                nc.sync.dma_start(
-                    out=w_scales[run][32 * b + r : P : 64].bitcast(I32),
-                    in_=scales_dram[gs, 4 * b + r : 16 : 8, :].rearrange("g s n -> s g n"),
-                )
+        def load_h(i):
+            g, n = UNITS[i]
+            nc.sync.dma_start(out=h_sb[i][:], in_=h_rows[:, :, g * K_PASS : (g + n) * K_PASS])
 
-        h_rows = h.rearrange("n o k -> n (o k)")
-        k_load = QUANT_PASSES * K_PASS
-        h_loads = ATOM_TILES * PASSES // QUANT_PASSES
-        for i in range(h_loads):
-            unit, m = divmod(i, ATOM_TILES)
-            ks = slice(unit * k_load, (unit + 1) * k_load)
-            nc.sync.dma_start(out=h_sb[:, m, ks], in_=h_rows[m * P : (m + 1) * P, ks])
-            if i >= h_loads - 4:
-                load_scale_rows(0, i - (h_loads - 4))
-
-        loads_a_run = SCALE_PASSES // WORD_PASSES
-        for i in range(PASSES // WORD_PASSES):
+        def load_words(i):
+            g, n = UNITS[i]
             nc.sync.dma_start(
                 out=w_words[i][:].bitcast(I32),
-                in_=words_dram[i * WORD_PASSES : (i + 1) * WORD_PASSES].rearrange("g p n -> p g n"),
+                in_=words_dram[g : g + n].rearrange("g p n -> p g n"),
             )
-            next_run = i // loads_a_run + 1
-            if next_run < PASSES // SCALE_PASSES:
-                load_scale_rows(next_run, i % loads_a_run)
-            if i == PASSES // WORD_PASSES // 2 - 1:
-                nc.sync.dma_start(
-                    out=mu_w_sb[:], in_=mu_W.rearrange("(m p) c f -> p m c f", p=P)
-                )
-                nc.sync.dma_start(out=mu_sb[:], in_=mu.rearrange("(m p) c f -> p m c f", p=P))
-                nc.sync.dma_start(
-                    out=mu_vw_sb[:], in_=mu_VW.rearrange("(m p) o f -> p m (o f)", p=P)
-                )
-                nc.sync.dma_start(out=q_sb[:], in_=q.rearrange("(m p) o f -> p m (o f)", p=P))
 
-        h_words = h_sb[:].bitcast(F32)
-        words_pass = K_PASS // 2
-        for unit in range(PASSES // QUANT_PASSES):
-            grouped = stage.tile([P, QUANT_PASSES, ATOMS, PACK], BF16, align_bytes=64)
-            grouped_words = grouped[:].bitcast(F32)
-            for j in range(QUANT_PASSES):
-                g = unit * QUANT_PASSES + j
-                flipped = banks.tile([P, PAIRS, ATOMS], F32, tag="bank")
+        def load_scales(run):
+            gs = slice(run * SCALE_PASSES, (run + 1) * SCALE_PASSES)
+            for r in range(4):
+                nc.sync.dma_start(
+                    out=w_scales[run][r:P:32].bitcast(I32),
+                    in_=scales_dram[gs, r:16:4, :].rearrange("g s n -> s g n"),
+                )
+
+        load_h(0)
+        for i, (g, n) in enumerate(UNITS):
+            if i + 1 < len(UNITS):
+                load_h(i + 1)
+            if g % SCALE_PASSES == 0:
+                load_scales(g // SCALE_PASSES)
+            load_words(i)
+            if i == len(UNITS) - 4:
+                nc.sync.dma_start(out=mu_w_sb[:], in_=mu_W.rearrange("(p m) c f -> p m c f", p=P))
+                nc.sync.dma_start(out=mu_sb[:], in_=mu.rearrange("(p m) c f -> p m c f", p=P))
+                nc.sync.dma_start(
+                    out=mu_vw_sb[:], in_=mu_VW.rearrange("(p m) o f -> p m (o f)", p=P)
+                )
+                nc.sync.dma_start(out=q_sb[:], in_=q.rearrange("(p m) o f -> p m (o f)", p=P))
+
+        def spread_bias():
+            for first, last in ((0, F), (F, COLS)):
+                bank = flip_banks.tile([P, last - first], F32, tag="flip", name="bias_%d" % first)
+                nc.tensor.matmul(
+                    out=bank[:], lhsT=ones[:], rhs=bias_rows[:, first:last], start=True, stop=True
+                )
+                nc.scalar.copy(out=bias[:, first:last], in_=bank[:])
+
+        sorted_words = {}
+        grouped = {}
+        flipped = {}
+        h_codes = {}
+        h_scales = {}
+        wide_sum = [
+            sum_banks.tile([P, WIDE], F32, name="wide_sum_%d" % m) for m in range(ATOM_TILES)
+        ]
+        narrow_bank = sum_banks.tile([P, ATOM_TILES, F], F32)
+
+        def sort_words(i):
+            n = UNITS[i][1]
+            sorted_words[i] = stage.tile(
+                [P, ATOM_TILES * n, PAIRS, P], F32, tag="sorted", name="sorted_%d" % i
+            )
+            nc.vector.tensor_copy(
+                out=sorted_words[i][:],
+                in_=h_sb[i][:]
+                .rearrange("p m k -> p (m k)")
+                .bitcast(F32)
+                .rearrange("p (n w u) -> p n u w", w=P, u=PAIRS),
+            )
+
+        def flip(i):
+            n = UNITS[i][1]
+            flipped[i] = []
+            for j in range(n):
+                bank = flip_banks.tile(
+                    [P, PAIRS, ATOMS], F32, tag="flip", name="flipped_%d_%d" % (i, j)
+                )
+                flipped[i].append(bank)
                 for u in range(PAIRS):
                     for m in range(ATOM_TILES):
                         nc.tensor.transpose(
-                            flipped[:, u, m * P : (m + 1) * P],
-                            h_words[:, m, words_pass * g + u : words_pass * (g + 1) : PAIRS],
+                            bank[:, u, m * P : (m + 1) * P],
+                            sorted_words[i][:, m * n + j, u, :],
                             identity[:],
                         )
-                together = flipped[:].rearrange("p u a -> p a u")
-                if j == QUANT_PASSES - 1:
-                    nc.vector.tensor_copy(out=grouped_words[:, j], in_=together)
-                else:
-                    nc.scalar.copy(out=grouped_words[:, j], in_=together)
-            gs = slice(unit * QUANT_PASSES, (unit + 1) * QUANT_PASSES)
+
+        def group(i):
+            n = UNITS[i][1]
+            grouped[i] = stage.tile(
+                [P, n, ATOMS, PACK], BF16, align_bytes=64, tag="grouped", name="grouped_%d" % i
+            )
+            words = grouped[i][:].bitcast(F32)
+            for j in range(n):
+                nc.scalar.copy(out=words[:, j], in_=flipped[i][j][:].rearrange("p u a -> p a u"))
+
+        def quantize(i):
+            n = UNITS[i][1]
+            h_codes[i] = stage.tile(
+                [P, n, ATOMS], U32, align_bytes=64, tag="h_codes", name="h_codes_%d" % i
+            )
+            h_scales[i] = stage.tile(
+                [P, n, ATOMS], U8, align_bytes=64, tag="h_scales", name="h_scales_%d" % i
+            )
             nc.vector.quantize_mx(
-                out=h_codes[:, gs, :].rearrange("p g a -> p (g a)").bitcast(FP8X4),
-                scales=h_scales[:, gs, :].rearrange("p g a -> p (g a)"),
-                in_=grouped[:].rearrange("p g a t -> p (g a t)"),
+                out=h_codes[i][:].rearrange("p g a -> p (g a)").bitcast(FP8X4),
+                scales=h_scales[i][:].rearrange("p g a -> p (g a)"),
+                in_=grouped[i][:].rearrange("p g a t -> p (g a t)"),
             )
 
-        bias_wide = bias_banks.tile([P, WIDE[1]], F32)
-        bias_narrow = bias_banks.tile([P, COLS - WIDE[1]], F32)
-        nc.tensor.matmul(
-            out=bias_wide[:], lhsT=ones[:], rhs=bias_rows[:, : WIDE[1]], start=True, stop=True
-        )
-        nc.tensor.matmul(
-            out=bias_narrow[:], lhsT=ones[:], rhs=bias_rows[:, WIDE[1] :], start=True, stop=True
-        )
-
-        nc.vector.tensor_tensor(
-            out=base_mu[:].rearrange("p m c f -> p (m c) f"),
-            in0=mu_w_sb[:].rearrange("p m c f -> p (m c) f"),
-            in1=bias_wide[:, F : 2 * F].unsqueeze(1).to_broadcast([P, ATOM_TILES * AXES, F]),
-            op=MULT,
-        )
-        nc.vector.tensor_tensor(out=base_mu[:], in0=base_mu[:], in1=mu_sb[:], op=ADD)
-        nc.vector.tensor_tensor(
-            out=base_q[:],
-            in0=mu_vw_sb[:],
-            in1=bias_narrow[:].unsqueeze(1).to_broadcast([P, ATOM_TILES, F]),
-            op=MULT,
-        )
-        nc.vector.tensor_tensor(
-            out=base_q[:],
-            in0=base_q[:],
-            in1=bias_wide[:, :F].unsqueeze(1).to_broadcast([P, ATOM_TILES, F]),
-            op=ADD,
-        )
-        nc.vector.tensor_tensor(out=base_q[:], in0=base_q[:], in1=q_sb[:], op=ADD)
-
-        sums = {}
-        for m in range(ATOM_TILES):
-            for block in (WIDE,) + NARROW:
-                sums[(m, block)] = banks.tile(
-                    [P, block[1]], F32, tag="bank", name="sum_%d_%d" % (m, block[0])
-                )
-
-        def mx_pass(g, m, block):
-            first, width = block
+        def mx_pass(i, j, m, out, first, width, start, stop):
+            g = UNITS[i][0] + j
             atoms = slice(m * P, (m + 1) * P)
             nc.tensor.matmul_mx(
-                out=sums[(m, block)][:],
-                lhsT=h_codes[:, g, atoms].bitcast(FP8X4),
-                lhsT_scale=h_scales[:, g, atoms],
-                rhs=w_words[g // WORD_PASSES][
-                    :, g % WORD_PASSES, 2 * first : 2 * (first + width)
-                ].bitcast(FP4X4),
+                out=out,
+                lhsT=h_codes[i][:, j, atoms].bitcast(FP8X4),
+                lhsT_scale=h_scales[i][:, j, atoms],
+                rhs=w_words[i][:, j, 2 * first : 2 * (first + width)].bitcast(FP4X4),
                 rhs_scale=w_scales[g // SCALE_PASSES][:, g % SCALE_PASSES, first : first + width],
-                start=(g == 0),
-                stop=(g == PASSES - 1),
+                start=start,
+                stop=stop,
             )
 
-        for g in range(PASSES - LAST_RUN):
-            for m in range(ATOM_TILES):
-                for block in (WIDE,) + NARROW:
-                    mx_pass(g, m, block)
-        last_passes = range(PASSES - LAST_RUN, PASSES)
-        for m in range(ATOM_TILES):
-            for g in last_passes:
-                mx_pass(g, m, WIDE)
-        for m in range(ATOM_TILES):
-            for block in NARROW:
-                for g in last_passes:
-                    mx_pass(g, m, block)
+        def multiply_wide(i, m):
+            g, n = UNITS[i]
+            for j in range(n):
+                mx_pass(i, j, m, wide_sum[m][:], F, WIDE, g + j == 0, g + j == PASSES - 1)
 
+        def multiply_narrow(units, m):
+            passes = [(i, j) for i in units for j in range(UNITS[i][1])]
+            for first in range(0, F, NARROW):
+                for i, j in passes:
+                    mx_pass(
+                        i, j, m, narrow_bank[:, m, first : first + NARROW], first, NARROW,
+                        (i, j) == passes[0], (i, j) == passes[-1],
+                    )
+
+        def keep_narrow(i):
+            if i == 0:
+                nc.vector.tensor_copy(out=narrow_sum[:], in_=narrow_bank[:])
+            else:
+                nc.vector.tensor_tensor(
+                    out=narrow_sum[:], in0=narrow_bank[:], in1=narrow_sum[:], op=ADD
+                )
+
+        def make_base_mu():
+            nc.vector.tensor_tensor(
+                out=base_mu[:].rearrange("p m c f -> p (m c) f"),
+                in0=mu_w_sb[:].rearrange("p m c f -> p (m c) f"),
+                in1=bias[:, F : 2 * F].unsqueeze(1).to_broadcast([P, ATOM_TILES * AXES, F]),
+                op=MULT,
+            )
+            nc.vector.tensor_tensor(out=base_mu[:], in0=base_mu[:], in1=mu_sb[:], op=ADD)
+
+        def make_base_q():
+            nc.vector.tensor_tensor(
+                out=base_q[:],
+                in0=mu_vw_sb[:],
+                in1=bias[:, 2 * F :].unsqueeze(1).to_broadcast([P, ATOM_TILES, F]),
+                op=MULT,
+            )
+            nc.vector.tensor_tensor(
+                out=gate[:],
+                in0=q_sb[:],
+                in1=bias[:, :F].unsqueeze(1).to_broadcast([P, ATOM_TILES, F]),
+                op=ADD,
+            )
+            nc.vector.tensor_tensor(out=base_q[:], in0=base_q[:], in1=narrow_sum[:], op=ADD)
+            nc.vector.tensor_tensor(out=base_q[:], in0=base_q[:], in1=gate[:], op=ADD)
+
+        last = len(UNITS) - 1
+        sort_words(0)
+        sort_words(1)
+        flip(0)
+        group(0)
+        quantize(0)
+        for i in range(last):
+            if i + 2 <= last:
+                sort_words(i + 2)
+            flip(i + 1)
+            group(i + 1)
+            quantize(i + 1)
+            if i == 0:
+                spread_bias()
+            if i not in TAIL_UNITS:
+                for m in range(ATOM_TILES):
+                    multiply_wide(i, m)
+                for m in range(ATOM_TILES):
+                    multiply_narrow([i], m)
+                keep_narrow(i)
+            if i == last - 2:
+                make_base_mu()
+        make_base_q()
+
+        out_mu = out_1.rearrange("(p m) c f -> p m (c f)", p=P)
+        out_q = out_0.rearrange("(p m) o f -> p m (o f)", p=P)
         for m in range(ATOM_TILES):
-            wide = sums[(m, WIDE)]
+            for i in TAIL_UNITS:
+                multiply_wide(i, m)
+            multiply_narrow(TAIL_UNITS, m)
             nc.vector.tensor_tensor(
                 out=mu_new[:, m],
                 in0=mu_w_sb[:, m],
-                in1=wide[:, F : 2 * F].unsqueeze(1).to_broadcast([P, AXES, F]),
+                in1=wide_sum[m][:, :F].unsqueeze(1).to_broadcast([P, AXES, F]),
                 op=MULT,
             )
-            nc.vector.tensor_tensor(out=q_new[:, m], in0=base_q[:, m], in1=wide[:, :F], op=ADD)
+            nc.vector.tensor_tensor(
+                out=gate[:, m], in0=mu_vw_sb[:, m], in1=wide_sum[m][:, F:], op=MULT
+            )
             nc.vector.tensor_tensor(
                 out=mu_new[:, m], in0=mu_new[:, m], in1=base_mu[:, m], op=ADD
             )
             nc.sync.dma_start(
-                out=out_1[m * P : (m + 1) * P].rearrange("n c f -> n (c f)"),
-                in_=mu_new[:, m].rearrange("p c f -> p (c f)"),
+                out=out_mu[:, m], in_=mu_new[:, m].rearrange("p c f -> p (c f)")
             )
-        for m in range(ATOM_TILES):
-            for block in NARROW:
-                cols = slice(block[0] - 2 * F, block[0] - 2 * F + block[1])
-                nc.vector.tensor_tensor(
-                    out=gate[:, m, cols],
-                    in0=mu_vw_sb[:, m, cols],
-                    in1=sums[(m, block)][:],
-                    op=MULT,
-                )
-            nc.vector.tensor_tensor(out=q_new[:, m], in0=q_new[:, m], in1=gate[:, m], op=ADD)
-            nc.sync.dma_start(
-                out=out_0[m * P : (m + 1) * P].rearrange("n o f -> n (o f)"), in_=q_new[:, m]
+            nc.vector.tensor_tensor(out=gate[:, m], in0=gate[:, m], in1=base_q[:, m], op=ADD)
+            nc.vector.tensor_tensor(
+                out=q_new[:, m], in0=narrow_bank[:, m], in1=gate[:, m], op=ADD
             )
+            nc.sync.dma_start(out=out_q[:, m], in_=q_new[:, m])

@@ -28,7 +28,7 @@ WIDE = 512
 
 UNITS = [(0, 2), (2, 2)] + [(g, 4) for g in range(4, PASSES, 4)]
 TAIL_UNITS = (len(UNITS) - 2, len(UNITS) - 1)
-SCALE_PASSES = 8
+SCALE_PASSES = 16
 
 FLOPS = 2 * ATOMS * K * COLS
 
@@ -94,21 +94,35 @@ def tile_painnmixing_pb_k_kernel(
                 in_=words_dram[g : g + n].rearrange("g p n -> p g n"),
             )
 
-        def load_scales(run):
+        def load_scale_row(run, q4, r):
             gs = slice(run * SCALE_PASSES, (run + 1) * SCALE_PASSES)
-            for r in range(4):
-                nc.sync.dma_start(
-                    out=w_scales[run][r:P:32].bitcast(I32),
-                    in_=scales_dram[gs, r:16:4, :].rearrange("g s n -> s g n"),
-                )
+            part = 32 * q4 + r
+            nc.sync.dma_start(
+                out=w_scales[run][part : part + 1].bitcast(I32),
+                in_=scales_dram[gs, 4 * q4 + r : 4 * q4 + r + 1, :].rearrange("g s n -> s g n"),
+            )
+
+        scale_rows = [(q4, r) for r in range(4) for q4 in (0, 2, 1, 3)]
+        later_rows = list(scale_rows)
+
+        def load_some_scales(count):
+            for q4, r in later_rows[:count]:
+                load_scale_row(1, q4, r)
+            for row in later_rows[:count]:
+                later_rows.remove(row)
 
         load_h(0)
         for i, (g, n) in enumerate(UNITS):
             if i + 1 < len(UNITS):
                 load_h(i + 1)
-            if g % SCALE_PASSES == 0:
-                load_scales(g // SCALE_PASSES)
+            if i == 0:
+                for q4, r in scale_rows:
+                    load_scale_row(0, q4, r)
+            else:
+                load_some_scales(3)
             load_words(i)
+            if i > 0:
+                load_some_scales(3)
             if i == len(UNITS) - 4:
                 nc.sync.dma_start(out=mu_w_sb[:], in_=mu_W.rearrange("(p m) c f -> p m c f", p=P))
                 nc.sync.dma_start(out=mu_sb[:], in_=mu.rearrange("(p m) c f -> p m c f", p=P))

@@ -26,9 +26,13 @@ COLS = 3 * F
 NARROW = 128
 WIDE = 512
 
-UNITS = [(0, 2), (2, 2)] + [(g, 4) for g in range(4, PASSES, 4)]
-TAIL_UNITS = (len(UNITS) - 2, len(UNITS) - 1)
-SCALE_PASSES = 16
+STEP = 2
+STEPS = PASSES // STEP
+TAIL_STEPS = range(STEPS - 4, STEPS)
+
+H_LOADS = [(0, 2), (2, 2)] + [(g, 4) for g in range(4, PASSES, 4)]
+W_LOADS = [(g, 4) for g in range(0, PASSES, 4)]
+SCALE_RUNS = [(0, 8, 4), (8, 16, 1), (24, 8, 4)]
 
 FLOPS = 2 * ATOMS * K * COLS
 
@@ -40,20 +44,21 @@ def tile_painnmixing_pb_k_kernel(
     with (
         tc.tile_pool(name="keep", bufs=1) as keep,
         tc.tile_pool(name="stage", bufs=3) as stage,
+        tc.tile_pool(name="code_tiles", bufs=5) as code_tiles,
         tc.psum_pool(name="sum_banks", bufs=1) as sum_banks,
-        tc.psum_pool(name="flip_banks", bufs=5) as flip_banks,
+        tc.psum_pool(name="flip_banks", bufs=4) as flip_banks,
         tc.manual_schedule(),
     ):
         h_sb = [
-            keep.tile([P, ATOM_TILES, n * K_PASS], BF16, name="h_%d" % g) for g, n in UNITS
+            keep.tile([P, ATOM_TILES, n * K_PASS], BF16, name="h_%d" % g) for g, n in H_LOADS
         ]
         w_words = [
             keep.tile([P, n, 2 * COLS], U8, align_bytes=64, name="w_words_%d" % g)
-            for g, n in UNITS
+            for g, n in W_LOADS
         ]
         w_scales = [
-            keep.tile([P, SCALE_PASSES, COLS], U8, align_bytes=64, name="w_scales_%d" % i)
-            for i in range(PASSES // SCALE_PASSES)
+            keep.tile([P, n, COLS], U8, align_bytes=64, name="w_scales_%d" % g)
+            for g, n, parts in SCALE_RUNS
         ]
         identity = keep.tile([P, P], F32)
         ones = keep.tile([P, P], BF16)
@@ -84,46 +89,49 @@ def tile_painnmixing_pb_k_kernel(
         h_rows = h.rearrange("(p m) o k -> p m (o k)", p=P)
 
         def load_h(i):
-            g, n = UNITS[i]
+            g, n = H_LOADS[i]
             nc.sync.dma_start(out=h_sb[i][:], in_=h_rows[:, :, g * K_PASS : (g + n) * K_PASS])
 
         def load_words(i):
-            g, n = UNITS[i]
+            g, n = W_LOADS[i]
             nc.sync.dma_start(
                 out=w_words[i][:].bitcast(I32),
                 in_=words_dram[g : g + n].rearrange("g p n -> p g n"),
             )
 
-        def load_scale_row(run, q4, r):
-            gs = slice(run * SCALE_PASSES, (run + 1) * SCALE_PASSES)
-            part = 32 * q4 + r
+        def load_scales(run, first):
+            g, n, parts = SCALE_RUNS[run]
+            if parts == 4:
+                q4, r = 0, first
+            else:
+                q4, r = (0, 2, 1, 3)[first % 4], first // 4
+            part, row = 32 * q4 + r, 4 * q4 + r
             nc.sync.dma_start(
-                out=w_scales[run][part : part + 1].bitcast(I32),
-                in_=scales_dram[gs, 4 * q4 + r : 4 * q4 + r + 1, :].rearrange("g s n -> s g n"),
+                out=w_scales[run][part : part + 32 * parts - 31 : 32].bitcast(I32),
+                in_=scales_dram[g : g + n, row : row + 4 * parts - 3 : 4, :].rearrange(
+                    "g s n -> s g n"
+                ),
             )
 
-        scale_rows = [(q4, r) for r in range(4) for q4 in (0, 2, 1, 3)]
-        later_rows = list(scale_rows)
-
         def load_some_scales(count):
-            for q4, r in later_rows[:count]:
-                load_scale_row(1, q4, r)
-            for row in later_rows[:count]:
-                later_rows.remove(row)
+            for run, first in scale_loads[:count]:
+                load_scales(run, first)
+            for done in scale_loads[:count]:
+                scale_loads.remove(done)
 
-        load_h(0)
-        for i, (g, n) in enumerate(UNITS):
-            if i + 1 < len(UNITS):
-                load_h(i + 1)
-            if i == 0:
-                for q4, r in scale_rows:
-                    load_scale_row(0, q4, r)
-            else:
-                load_some_scales(3)
+        scale_loads = [
+            (run, first) for run in range(len(SCALE_RUNS)) for first in range(16 // SCALE_RUNS[run][2])
+        ]
+        for i in range(2):
+            load_h(i)
+        load_some_scales(4)
+        load_words(0)
+        for i in range(1, len(W_LOADS)):
+            load_h(i + 1)
+            load_some_scales(2)
             load_words(i)
-            if i > 0:
-                load_some_scales(3)
-            if i == len(UNITS) - 4:
+            load_some_scales(3)
+            if i == len(W_LOADS) - 4:
                 nc.sync.dma_start(out=mu_w_sb[:], in_=mu_W.rearrange("(p m) c f -> p m c f", p=P))
                 nc.sync.dma_start(out=mu_sb[:], in_=mu.rearrange("(p m) c f -> p m c f", p=P))
                 nc.sync.dma_start(
@@ -147,150 +155,177 @@ def tile_painnmixing_pb_k_kernel(
         wide_sum = [
             sum_banks.tile([P, WIDE], F32, name="wide_sum_%d" % m) for m in range(ATOM_TILES)
         ]
-        narrow_bank = sum_banks.tile([P, ATOM_TILES, F], F32)
+        narrow_bank = [
+            sum_banks.tile([P, F], F32, name="narrow_sum_%d" % m) for m in range(ATOM_TILES)
+        ]
 
         def sort_words(i):
-            n = UNITS[i][1]
-            sorted_words[i] = stage.tile(
+            g, n = H_LOADS[i]
+            words = stage.tile(
                 [P, ATOM_TILES * n, PAIRS, P], F32, tag="sorted", name="sorted_%d" % i
             )
             nc.vector.tensor_copy(
-                out=sorted_words[i][:],
+                out=words[:],
                 in_=h_sb[i][:]
                 .rearrange("p m k -> p (m k)")
                 .bitcast(F32)
                 .rearrange("p (n w u) -> p n u w", w=P, u=PAIRS),
             )
-
-        def flip(i):
-            n = UNITS[i][1]
-            flipped[i] = []
             for j in range(n):
-                bank = flip_banks.tile(
-                    [P, PAIRS, ATOMS], F32, tag="flip", name="flipped_%d_%d" % (i, j)
+                for m in range(ATOM_TILES):
+                    sorted_words[(g + j, m)] = words[:, m * n + j]
+
+        def flip(step):
+            for g in range(step * STEP, (step + 1) * STEP):
+                flipped[g] = flip_banks.tile(
+                    [P, PAIRS, ATOMS], F32, tag="flip", name="flipped_%d" % g
                 )
-                flipped[i].append(bank)
                 for u in range(PAIRS):
                     for m in range(ATOM_TILES):
                         nc.tensor.transpose(
-                            bank[:, u, m * P : (m + 1) * P],
-                            sorted_words[i][:, m * n + j, u, :],
+                            flipped[g][:, u, m * P : (m + 1) * P],
+                            sorted_words[(g, m)][:, u, :],
                             identity[:],
                         )
 
-        def group(i):
-            n = UNITS[i][1]
-            grouped[i] = stage.tile(
-                [P, n, ATOMS, PACK], BF16, align_bytes=64, tag="grouped", name="grouped_%d" % i
+        def group(step):
+            grouped[step] = stage.tile(
+                [P, STEP, ATOMS, PACK], BF16, align_bytes=64, tag="grouped",
+                name="grouped_%d" % step,
             )
-            words = grouped[i][:].bitcast(F32)
-            for j in range(n):
-                nc.scalar.copy(out=words[:, j], in_=flipped[i][j][:].rearrange("p u a -> p a u"))
+            words = grouped[step][:].bitcast(F32)
+            for j in range(STEP):
+                nc.scalar.copy(
+                    out=words[:, j], in_=flipped[step * STEP + j][:].rearrange("p u a -> p a u")
+                )
 
-        def quantize(i):
-            n = UNITS[i][1]
-            h_codes[i] = stage.tile(
-                [P, n, ATOMS], U32, align_bytes=64, tag="h_codes", name="h_codes_%d" % i
+        def quantize(step):
+            codes = code_tiles.tile(
+                [P, STEP, ATOMS], U32, align_bytes=64, tag="codes", name="codes_%d" % step
             )
-            h_scales[i] = stage.tile(
-                [P, n, ATOMS], U8, align_bytes=64, tag="h_scales", name="h_scales_%d" % i
+            scales = code_tiles.tile(
+                [P, STEP, ATOMS], U8, align_bytes=64, tag="scales", name="scales_%d" % step
             )
             nc.vector.quantize_mx(
-                out=h_codes[i][:].rearrange("p g a -> p (g a)").bitcast(FP8X4),
-                scales=h_scales[i][:].rearrange("p g a -> p (g a)"),
-                in_=grouped[i][:].rearrange("p g a t -> p (g a t)"),
+                out=codes[:].rearrange("p g a -> p (g a)").bitcast(FP8X4),
+                scales=scales[:].rearrange("p g a -> p (g a)"),
+                in_=grouped[step][:].rearrange("p g a t -> p (g a t)"),
             )
+            for j in range(STEP):
+                h_codes[step * STEP + j] = codes[:, j]
+                h_scales[step * STEP + j] = scales[:, j]
 
-        def mx_pass(i, j, m, out, first, width, start, stop):
-            g = UNITS[i][0] + j
+        def mx_pass(g, m, out, first, width, start, stop):
             atoms = slice(m * P, (m + 1) * P)
+            load = [i for i in range(len(W_LOADS)) if W_LOADS[i][0] <= g][-1]
+            run = [i for i in range(len(SCALE_RUNS)) if SCALE_RUNS[i][0] <= g][-1]
             nc.tensor.matmul_mx(
                 out=out,
-                lhsT=h_codes[i][:, j, atoms].bitcast(FP8X4),
-                lhsT_scale=h_scales[i][:, j, atoms],
-                rhs=w_words[i][:, j, 2 * first : 2 * (first + width)].bitcast(FP4X4),
-                rhs_scale=w_scales[g // SCALE_PASSES][:, g % SCALE_PASSES, first : first + width],
+                lhsT=h_codes[g][:, atoms].bitcast(FP8X4),
+                lhsT_scale=h_scales[g][:, atoms],
+                rhs=w_words[load][
+                    :, g - W_LOADS[load][0], 2 * first : 2 * (first + width)
+                ].bitcast(FP4X4),
+                rhs_scale=w_scales[run][:, g - SCALE_RUNS[run][0], first : first + width],
                 start=start,
                 stop=stop,
             )
 
-        def multiply_wide(i, m):
-            g, n = UNITS[i]
-            for j in range(n):
-                mx_pass(i, j, m, wide_sum[m][:], F, WIDE, g + j == 0, g + j == PASSES - 1)
+        def multiply_wide(passes, m):
+            for g in passes:
+                mx_pass(g, m, wide_sum[m][:], F, WIDE, g == 0, g == PASSES - 1)
 
-        def multiply_narrow(units, m):
-            passes = [(i, j) for i in units for j in range(UNITS[i][1])]
+        def multiply_narrow(passes, m):
             for first in range(0, F, NARROW):
-                for i, j in passes:
+                for g in passes:
                     mx_pass(
-                        i, j, m, narrow_bank[:, m, first : first + NARROW], first, NARROW,
-                        (i, j) == passes[0], (i, j) == passes[-1],
+                        g, m, narrow_bank[m][:, first : first + NARROW], first, NARROW,
+                        g == passes[0], g == passes[-1],
                     )
 
-        def keep_narrow(i):
-            if i == 0:
-                nc.vector.tensor_copy(out=narrow_sum[:], in_=narrow_bank[:])
+        def keep_narrow(first, m):
+            if first:
+                nc.vector.tensor_copy(out=narrow_sum[:, m], in_=narrow_bank[m][:])
             else:
                 nc.vector.tensor_tensor(
-                    out=narrow_sum[:], in0=narrow_bank[:], in1=narrow_sum[:], op=ADD
+                    out=narrow_sum[:, m], in0=narrow_bank[m][:], in1=narrow_sum[:, m], op=ADD
                 )
 
-        def make_base_mu():
-            nc.vector.tensor_tensor(
-                out=base_mu[:].rearrange("p m c f -> p (m c) f"),
-                in0=mu_w_sb[:].rearrange("p m c f -> p (m c) f"),
-                in1=bias[:, F : 2 * F].unsqueeze(1).to_broadcast([P, ATOM_TILES * AXES, F]),
-                op=MULT,
-            )
-            nc.vector.tensor_tensor(out=base_mu[:], in0=base_mu[:], in1=mu_sb[:], op=ADD)
+        def make_base_mu(m, op):
+            if op == MULT:
+                nc.vector.tensor_tensor(
+                    out=base_mu[:, m],
+                    in0=mu_w_sb[:, m],
+                    in1=bias[:, F : 2 * F].unsqueeze(1).to_broadcast([P, AXES, F]),
+                    op=MULT,
+                )
+            else:
+                nc.vector.tensor_tensor(
+                    out=base_mu[:, m], in0=base_mu[:, m], in1=mu_sb[:, m], op=ADD
+                )
 
-        def make_base_q():
-            nc.vector.tensor_tensor(
-                out=base_q[:],
-                in0=mu_vw_sb[:],
-                in1=bias[:, 2 * F :].unsqueeze(1).to_broadcast([P, ATOM_TILES, F]),
-                op=MULT,
-            )
-            nc.vector.tensor_tensor(
-                out=gate[:],
-                in0=q_sb[:],
-                in1=bias[:, :F].unsqueeze(1).to_broadcast([P, ATOM_TILES, F]),
-                op=ADD,
-            )
-            nc.vector.tensor_tensor(out=base_q[:], in0=base_q[:], in1=narrow_sum[:], op=ADD)
-            nc.vector.tensor_tensor(out=base_q[:], in0=base_q[:], in1=gate[:], op=ADD)
+        def make_base_q(op):
+            if op == MULT:
+                nc.vector.tensor_tensor(
+                    out=base_q[:],
+                    in0=mu_vw_sb[:],
+                    in1=bias[:, 2 * F :].unsqueeze(1).to_broadcast([P, ATOM_TILES, F]),
+                    op=MULT,
+                )
+                nc.vector.tensor_tensor(
+                    out=gate[:],
+                    in0=q_sb[:],
+                    in1=bias[:, :F].unsqueeze(1).to_broadcast([P, ATOM_TILES, F]),
+                    op=ADD,
+                )
+            else:
+                nc.vector.tensor_tensor(out=base_q[:], in0=base_q[:], in1=gate[:], op=ADD)
+                nc.vector.tensor_tensor(out=base_q[:], in0=base_q[:], in1=narrow_sum[:], op=ADD)
 
-        last = len(UNITS) - 1
+        sort_at = {g // STEP - 4: i for i, (g, n) in enumerate(H_LOADS)}
         sort_words(0)
         sort_words(1)
         flip(0)
         group(0)
         quantize(0)
-        for i in range(last):
-            if i + 2 <= last:
-                sort_words(i + 2)
-            flip(i + 1)
-            group(i + 1)
-            quantize(i + 1)
-            if i == 0:
+        flip(1)
+        group(1)
+        quantize(1)
+        sort_words(2)
+        for step in range(STEPS):
+            for ahead in {0: (), 1: (2, 3)}.get(step, (step + 2,)):
+                if ahead < STEPS:
+                    flip(ahead)
+                    group(ahead)
+            if 1 < step + 1 < STEPS:
+                quantize(step + 1)
+            if step == 0:
                 spread_bias()
-            if i not in TAIL_UNITS:
+            if step in sort_at:
+                sort_words(sort_at[step])
+            if step in (STEPS - 6, STEPS - 5):
+                make_base_mu(step - (STEPS - 6), MULT)
+            if step in (STEPS - 4, STEPS - 3):
+                make_base_mu(step - (STEPS - 4), ADD)
+            if step == STEPS - 2:
+                make_base_q(MULT)
+            if step in TAIL_STEPS[:2]:
+                multiply_wide(range(step * STEP, (step + 1) * STEP), 0)
+            if step not in TAIL_STEPS:
                 for m in range(ATOM_TILES):
-                    multiply_wide(i, m)
-                for m in range(ATOM_TILES):
-                    multiply_narrow([i], m)
-                keep_narrow(i)
-            if i == last - 2:
-                make_base_mu()
-        make_base_q()
+                    multiply_wide(range(step * STEP, (step + 1) * STEP), m)
+                if step % 2 == 1:
+                    for m in range(ATOM_TILES):
+                        multiply_narrow(range((step - 1) * STEP, (step + 1) * STEP), m)
+                        keep_narrow(step == 1, m)
+        make_base_q(ADD)
 
         out_mu = out_1.rearrange("(p m) c f -> p m (c f)", p=P)
         out_q = out_0.rearrange("(p m) o f -> p m (o f)", p=P)
+        tail_passes = range(TAIL_STEPS[0] * STEP, PASSES)
         for m in range(ATOM_TILES):
-            for i in TAIL_UNITS:
-                multiply_wide(i, m)
-            multiply_narrow(TAIL_UNITS, m)
+            multiply_wide(tail_passes if m else tail_passes[2 * STEP :], m)
+            multiply_narrow(tail_passes, m)
             nc.vector.tensor_tensor(
                 out=mu_new[:, m],
                 in0=mu_w_sb[:, m],
@@ -308,6 +343,6 @@ def tile_painnmixing_pb_k_kernel(
             )
             nc.vector.tensor_tensor(out=gate[:, m], in0=gate[:, m], in1=base_q[:, m], op=ADD)
             nc.vector.tensor_tensor(
-                out=q_new[:, m], in0=narrow_bank[:, m], in1=gate[:, m], op=ADD
+                out=q_new[:, m], in0=narrow_bank[m][:], in1=gate[:, m], op=ADD
             )
             nc.sync.dma_start(out=out_q[:, m], in_=q_new[:, m])

@@ -26,13 +26,14 @@ COLS = 3 * F
 NARROW = 128
 WIDE = 512
 
-STEP = 2
-STEPS = PASSES // STEP
-TAIL_STEPS = range(STEPS - 4, STEPS)
+SIZES = [2] * 4 + [4] * 5 + [2] * 2
+UNITS = [(sum(SIZES[:i]), n) for i, n in enumerate(SIZES)]
+LAST = len(UNITS) - 1
+TAIL = (LAST - 2, LAST - 1, LAST)
+UNIT_OF_PASS = {g: i for i, (first, n) in enumerate(UNITS) for g in range(first, first + n)}
 
-H_LOADS = [(0, 2), (2, 2)] + [(g, 4) for g in range(4, PASSES, 4)]
-W_LOADS = [(g, 4) for g in range(0, PASSES, 4)]
-SCALE_RUNS = [(0, 8, 4), (8, 16, 1), (24, 8, 4)]
+RUN = 16
+RUNS = PASSES // RUN
 
 FLOPS = 2 * ATOMS * K * COLS
 
@@ -43,22 +44,22 @@ def tile_painnmixing_pb_k_kernel(
     nc = tc.nc
     with (
         tc.tile_pool(name="keep", bufs=1) as keep,
-        tc.tile_pool(name="stage", bufs=3) as stage,
-        tc.tile_pool(name="code_tiles", bufs=5) as code_tiles,
+        tc.tile_pool(name="stage", bufs=2) as stage,
+        tc.tile_pool(name="code_tiles", bufs=4) as code_tiles,
         tc.psum_pool(name="sum_banks", bufs=1) as sum_banks,
         tc.psum_pool(name="flip_banks", bufs=4) as flip_banks,
         tc.manual_schedule(),
     ):
         h_sb = [
-            keep.tile([P, ATOM_TILES, n * K_PASS], BF16, name="h_%d" % g) for g, n in H_LOADS
+            keep.tile([P, ATOM_TILES, n * K_PASS], BF16, name="h_%d" % g) for g, n in UNITS
         ]
         w_words = [
             keep.tile([P, n, 2 * COLS], U8, align_bytes=64, name="w_words_%d" % g)
-            for g, n in W_LOADS
+            for g, n in UNITS
         ]
         w_scales = [
-            keep.tile([P, n, COLS], U8, align_bytes=64, name="w_scales_%d" % g)
-            for g, n, parts in SCALE_RUNS
+            keep.tile([P, RUN, COLS], U8, align_bytes=64, name="w_scales_%d" % i)
+            for i in range(RUNS)
         ]
         identity = keep.tile([P, P], F32)
         ones = keep.tile([P, P], BF16)
@@ -68,19 +69,18 @@ def tile_painnmixing_pb_k_kernel(
         mu_sb = keep.tile([P, ATOM_TILES, AXES, F], BF16)
         mu_vw_sb = keep.tile([P, ATOM_TILES, F], BF16)
         q_sb = keep.tile([P, ATOM_TILES, F], BF16)
-        base_mu = keep.tile([P, ATOM_TILES, AXES, F], F32)
-        base_q = keep.tile([P, ATOM_TILES, F], F32)
+        factors = keep.tile([P, ATOM_TILES, WIDE], F32)
         narrow_sum = keep.tile([P, ATOM_TILES, F], F32)
         mu_new = keep.tile([P, ATOM_TILES, AXES, F], F32)
         q_new = keep.tile([P, ATOM_TILES, F], F32)
         gate = keep.tile([P, ATOM_TILES, F], F32)
 
-        nc.vector.memset(w_scales[0][:].bitcast(I32), 0)
+        half = RUN // 2
+        nc.vector.memset(w_scales[0][:, :half, :].bitcast(I32), 0)
+        nc.gpsimd.memset(w_scales[0][:, half:, :].bitcast(I32), 0)
         make_identity(nc, identity[:])
-        nc.gpsimd.memset(bias_rows[:], 0.0)
-        nc.gpsimd.memset(ones[:], 1.0)
-        for plane in w_scales[1:]:
-            nc.gpsimd.memset(plane[:].bitcast(I32), 0)
+        nc.vector.memset(bias_rows[:], 0.0)
+        nc.vector.memset(ones[:], 1.0)
 
         nc.scalar.dma_start(out=bias_rows[0:1, :], in_=b2.unsqueeze(0))
 
@@ -89,55 +89,55 @@ def tile_painnmixing_pb_k_kernel(
         h_rows = h.rearrange("(p m) o k -> p m (o k)", p=P)
 
         def load_h(i):
-            g, n = H_LOADS[i]
+            g, n = UNITS[i]
             nc.sync.dma_start(out=h_sb[i][:], in_=h_rows[:, :, g * K_PASS : (g + n) * K_PASS])
 
         def load_words(i):
-            g, n = W_LOADS[i]
+            g, n = UNITS[i]
             nc.sync.dma_start(
                 out=w_words[i][:].bitcast(I32),
                 in_=words_dram[g : g + n].rearrange("g p n -> p g n"),
             )
 
-        def load_scales(run, first):
-            g, n, parts = SCALE_RUNS[run]
-            if parts == 4:
-                q4, r = 0, first
-            else:
-                q4, r = (0, 2, 1, 3)[first % 4], first // 4
-            part, row = 32 * q4 + r, 4 * q4 + r
-            nc.sync.dma_start(
-                out=w_scales[run][part : part + 32 * parts - 31 : 32].bitcast(I32),
-                in_=scales_dram[g : g + n, row : row + 4 * parts - 3 : 4, :].rearrange(
-                    "g s n -> s g n"
-                ),
-            )
-
-        def load_some_scales(count):
-            for run, first in scale_loads[:count]:
-                load_scales(run, first)
-            for done in scale_loads[:count]:
-                scale_loads.remove(done)
-
-        scale_loads = [
-            (run, first) for run in range(len(SCALE_RUNS)) for first in range(16 // SCALE_RUNS[run][2])
-        ]
-        for i in range(2):
-            load_h(i)
-        load_some_scales(4)
-        load_words(0)
-        for i in range(1, len(W_LOADS)):
-            load_h(i + 1)
-            load_some_scales(2)
-            load_words(i)
-            load_some_scales(3)
-            if i == len(W_LOADS) - 4:
-                nc.sync.dma_start(out=mu_w_sb[:], in_=mu_W.rearrange("(p m) c f -> p m c f", p=P))
-                nc.sync.dma_start(out=mu_sb[:], in_=mu.rearrange("(p m) c f -> p m c f", p=P))
+        def load_scale_rows(run, first, count):
+            gs = slice(run * RUN, (run + 1) * RUN)
+            for i in range(first, min(first + count, 16)):
+                quadrant, r = (0, 2, 1, 3)[i % 4], i // 4
+                part, row = 32 * quadrant + r, 4 * quadrant + r
                 nc.sync.dma_start(
-                    out=mu_vw_sb[:], in_=mu_VW.rearrange("(p m) o f -> p m (o f)", p=P)
+                    out=w_scales[run][part : part + 1].bitcast(I32),
+                    in_=scales_dram[gs, row : row + 1, :].rearrange("g s n -> s g n"),
                 )
-                nc.sync.dma_start(out=q_sb[:], in_=q.rearrange("(p m) o f -> p m (o f)", p=P))
+
+        def load_factors():
+            nc.sync.dma_start(out=mu_w_sb[:], in_=mu_W.rearrange("(p m) c f -> p m c f", p=P))
+            nc.sync.dma_start(out=mu_sb[:], in_=mu.rearrange("(p m) c f -> p m c f", p=P))
+            nc.sync.dma_start(
+                out=mu_vw_sb[:], in_=mu_VW.rearrange("(p m) o f -> p m (o f)", p=P)
+            )
+            nc.sync.dma_start(out=q_sb[:], in_=q.rearrange("(p m) o f -> p m (o f)", p=P))
+
+        load_h(0)
+        load_scale_rows(0, 0, 5)
+        load_h(1)
+        load_scale_rows(0, 5, 5)
+        load_words(0)
+        load_scale_rows(0, 10, 6)
+        load_h(2)
+        load_words(1)
+        load_h(3)
+
+        def load_rest():
+            rows = 0
+            for i in range(2, LAST + 1):
+                load_words(i)
+                load_scale_rows(1, rows, 2)
+                if i + 2 <= LAST:
+                    load_h(i + 2)
+                    load_scale_rows(1, rows + 2, 2)
+                rows += 4
+                if i == LAST - 2:
+                    load_factors()
 
         def spread_bias():
             for first, last in ((0, F), (F, COLS)):
@@ -160,9 +160,9 @@ def tile_painnmixing_pb_k_kernel(
         ]
 
         def sort_words(i):
-            g, n = H_LOADS[i]
+            g, n = UNITS[i]
             words = stage.tile(
-                [P, ATOM_TILES * n, PAIRS, P], F32, tag="sorted", name="sorted_%d" % i
+                [P, ATOM_TILES * n, PAIRS, P], F32, tag="sorted", name="sorted_%d" % i, bufs=3
             )
             nc.vector.tensor_copy(
                 out=words[:],
@@ -175,8 +175,9 @@ def tile_painnmixing_pb_k_kernel(
                 for m in range(ATOM_TILES):
                     sorted_words[(g + j, m)] = words[:, m * n + j]
 
-        def flip(step):
-            for g in range(step * STEP, (step + 1) * STEP):
+        def flip(i):
+            first, n = UNITS[i]
+            for g in range(first, first + n):
                 flipped[g] = flip_banks.tile(
                     [P, PAIRS, ATOMS], F32, tag="flip", name="flipped_%d" % g
                 )
@@ -188,45 +189,43 @@ def tile_painnmixing_pb_k_kernel(
                             identity[:],
                         )
 
-        def group(step):
-            grouped[step] = stage.tile(
-                [P, STEP, ATOMS, PACK], BF16, align_bytes=64, tag="grouped",
-                name="grouped_%d" % step,
+        def group(i):
+            g, n = UNITS[i]
+            grouped[i] = stage.tile(
+                [P, n, ATOMS, PACK], BF16, align_bytes=64, tag="grouped", name="grouped_%d" % i
             )
-            words = grouped[step][:].bitcast(F32)
-            for j in range(STEP):
-                nc.scalar.copy(
-                    out=words[:, j], in_=flipped[step * STEP + j][:].rearrange("p u a -> p a u")
-                )
+            words = grouped[i][:].bitcast(F32)
+            for j in range(n):
+                nc.scalar.copy(out=words[:, j], in_=flipped[g + j][:].rearrange("p u a -> p a u"))
 
-        def quantize(step):
+        def quantize(i):
+            g, n = UNITS[i]
             codes = code_tiles.tile(
-                [P, STEP, ATOMS], U32, align_bytes=64, tag="codes", name="codes_%d" % step
+                [P, n, ATOMS], U32, align_bytes=64, tag="codes", name="codes_%d" % i
             )
             scales = code_tiles.tile(
-                [P, STEP, ATOMS], U8, align_bytes=64, tag="scales", name="scales_%d" % step
+                [P, n, ATOMS], U8, align_bytes=64, tag="scales", name="scales_%d" % i
             )
             nc.vector.quantize_mx(
                 out=codes[:].rearrange("p g a -> p (g a)").bitcast(FP8X4),
                 scales=scales[:].rearrange("p g a -> p (g a)"),
-                in_=grouped[step][:].rearrange("p g a t -> p (g a t)"),
+                in_=grouped[i][:].rearrange("p g a t -> p (g a t)"),
             )
-            for j in range(STEP):
-                h_codes[step * STEP + j] = codes[:, j]
-                h_scales[step * STEP + j] = scales[:, j]
+            for j in range(n):
+                h_codes[g + j] = codes[:, j]
+                h_scales[g + j] = scales[:, j]
 
         def mx_pass(g, m, out, first, width, start, stop):
             atoms = slice(m * P, (m + 1) * P)
-            load = [i for i in range(len(W_LOADS)) if W_LOADS[i][0] <= g][-1]
-            run = [i for i in range(len(SCALE_RUNS)) if SCALE_RUNS[i][0] <= g][-1]
+            unit = UNIT_OF_PASS[g]
             nc.tensor.matmul_mx(
                 out=out,
                 lhsT=h_codes[g][:, atoms].bitcast(FP8X4),
                 lhsT_scale=h_scales[g][:, atoms],
-                rhs=w_words[load][
-                    :, g - W_LOADS[load][0], 2 * first : 2 * (first + width)
+                rhs=w_words[unit][
+                    :, g - UNITS[unit][0], 2 * first : 2 * (first + width)
                 ].bitcast(FP4X4),
-                rhs_scale=w_scales[run][:, g - SCALE_RUNS[run][0], first : first + width],
+                rhs_scale=w_scales[g // RUN][:, g % RUN, first : first + width],
                 start=start,
                 stop=stop,
             )
@@ -244,104 +243,93 @@ def tile_painnmixing_pb_k_kernel(
                     )
 
         def keep_narrow(first, m):
-            if first:
-                nc.vector.tensor_copy(out=narrow_sum[:, m], in_=narrow_bank[m][:])
-            else:
-                nc.vector.tensor_tensor(
-                    out=narrow_sum[:, m], in0=narrow_bank[m][:], in1=narrow_sum[:, m], op=ADD
-                )
+            nc.vector.tensor_tensor(
+                out=narrow_sum[:, m],
+                in0=narrow_bank[m][:],
+                in1=bias[:, :F] if first else narrow_sum[:, m],
+                op=ADD,
+            )
 
-        def make_base_mu(m, op):
-            if op == MULT:
-                nc.vector.tensor_tensor(
-                    out=base_mu[:, m],
-                    in0=mu_w_sb[:, m],
-                    in1=bias[:, F : 2 * F].unsqueeze(1).to_broadcast([P, AXES, F]),
-                    op=MULT,
-                )
-            else:
-                nc.vector.tensor_tensor(
-                    out=base_mu[:, m], in0=base_mu[:, m], in1=mu_sb[:, m], op=ADD
-                )
+        def passes_of(units):
+            return [g for i in units for g in range(UNITS[i][0], UNITS[i][0] + UNITS[i][1])]
 
-        def make_base_q(op):
-            if op == MULT:
-                nc.vector.tensor_tensor(
-                    out=base_q[:],
-                    in0=mu_vw_sb[:],
-                    in1=bias[:, 2 * F :].unsqueeze(1).to_broadcast([P, ATOM_TILES, F]),
-                    op=MULT,
-                )
-                nc.vector.tensor_tensor(
-                    out=gate[:],
-                    in0=q_sb[:],
-                    in1=bias[:, :F].unsqueeze(1).to_broadcast([P, ATOM_TILES, F]),
-                    op=ADD,
-                )
-            else:
-                nc.vector.tensor_tensor(out=base_q[:], in0=base_q[:], in1=gate[:], op=ADD)
-                nc.vector.tensor_tensor(out=base_q[:], in0=base_q[:], in1=narrow_sum[:], op=ADD)
+        narrow_units = {}
+        waiting = []
+        for i in range(LAST + 1):
+            waiting.append(i)
+            if len(passes_of(waiting)) >= 4:
+                narrow_units[i] = waiting
+                waiting = []
+        sorted_to = [0]
+        ready = [0]
+        to_keep = []
 
-        sort_at = {g // STEP - 4: i for i, (g, n) in enumerate(H_LOADS)}
-        sort_words(0)
-        sort_words(1)
-        flip(0)
-        group(0)
-        quantize(0)
-        flip(1)
-        group(1)
-        quantize(1)
-        sort_words(2)
-        for step in range(STEPS):
-            for ahead in {0: (), 1: (2, 3)}.get(step, (step + 2,)):
-                if ahead < STEPS:
-                    flip(ahead)
-                    group(ahead)
-            if 1 < step + 1 < STEPS:
-                quantize(step + 1)
-            if step == 0:
-                spread_bias()
-            if step in sort_at:
-                sort_words(sort_at[step])
-            if step in (STEPS - 6, STEPS - 5):
-                make_base_mu(step - (STEPS - 6), MULT)
-            if step in (STEPS - 4, STEPS - 3):
-                make_base_mu(step - (STEPS - 4), ADD)
-            if step == STEPS - 2:
-                make_base_q(MULT)
-            if step in TAIL_STEPS[:2]:
-                multiply_wide(range(step * STEP, (step + 1) * STEP), 0)
-            if step not in TAIL_STEPS:
+        def sort_to(i):
+            while sorted_to[0] <= min(i, LAST):
+                sort_words(sorted_to[0])
+                sorted_to[0] += 1
+
+        def prepare(last_unit):
+            while ready[0] <= min(last_unit, LAST):
+                i = ready[0]
+                sort_to(LAST if i >= LAST - 2 else i + 1)
+                flip(i)
+                group(i)
+                quantize(i)
+                ready[0] += 1
+
+        def keep_waiting():
+            for i in to_keep:
                 for m in range(ATOM_TILES):
-                    multiply_wide(range(step * STEP, (step + 1) * STEP), m)
-                if step % 2 == 1:
+                    keep_narrow(narrow_units[i][0] == 0, m)
+            to_keep.clear()
+
+        sort_to(1)
+        nc.vector.memset(w_scales[1][:].bitcast(I32), 0)
+        load_rest()
+        prepare(0)
+        for i in range(LAST):
+            keep_waiting()
+            prepare(LAST if i + 2 >= LAST else i + 1)
+            if i not in TAIL:
+                for m in range(ATOM_TILES):
+                    multiply_wide(passes_of([i]), m)
+                if i in narrow_units:
                     for m in range(ATOM_TILES):
-                        multiply_narrow(range((step - 1) * STEP, (step + 1) * STEP), m)
-                        keep_narrow(step == 1, m)
-        make_base_q(ADD)
+                        multiply_narrow(passes_of(narrow_units[i]), m)
+                    to_keep.append(i)
+                if i == 0:
+                    spread_bias()
+        keep_waiting()
 
         out_mu = out_1.rearrange("(p m) c f -> p m (c f)", p=P)
         out_q = out_0.rearrange("(p m) o f -> p m (o f)", p=P)
-        tail_passes = range(TAIL_STEPS[0] * STEP, PASSES)
         for m in range(ATOM_TILES):
-            multiply_wide(tail_passes if m else tail_passes[2 * STEP :], m)
-            multiply_narrow(tail_passes, m)
+            multiply_wide(passes_of(TAIL[:1]), m)
+        for m in range(ATOM_TILES):
+            multiply_wide(passes_of(TAIL[1:]), m)
+        for m in range(ATOM_TILES):
+            multiply_narrow(passes_of(TAIL), m)
+        nc.vector.tensor_tensor(out=narrow_sum[:], in0=narrow_sum[:], in1=q_sb[:], op=ADD)
+        for m in range(ATOM_TILES):
+            nc.vector.tensor_tensor(
+                out=factors[:, m], in0=wide_sum[m][:], in1=bias[:, F:], op=ADD
+            )
             nc.vector.tensor_tensor(
                 out=mu_new[:, m],
                 in0=mu_w_sb[:, m],
-                in1=wide_sum[m][:, :F].unsqueeze(1).to_broadcast([P, AXES, F]),
+                in1=factors[:, m, :F].unsqueeze(1).to_broadcast([P, AXES, F]),
                 op=MULT,
             )
-            nc.vector.tensor_tensor(
-                out=gate[:, m], in0=mu_vw_sb[:, m], in1=wide_sum[m][:, F:], op=MULT
-            )
-            nc.vector.tensor_tensor(
-                out=mu_new[:, m], in0=mu_new[:, m], in1=base_mu[:, m], op=ADD
-            )
+        nc.vector.tensor_tensor(out=gate[:], in0=mu_vw_sb[:], in1=factors[:, :, F:], op=MULT)
+        for m in range(ATOM_TILES):
+            adder = nc.vector if m else nc.gpsimd
+            adder.tensor_tensor(out=mu_new[:, m], in0=mu_new[:, m], in1=mu_sb[:, m], op=ADD)
             nc.sync.dma_start(
                 out=out_mu[:, m], in_=mu_new[:, m].rearrange("p c f -> p (c f)")
             )
-            nc.vector.tensor_tensor(out=gate[:, m], in0=gate[:, m], in1=base_q[:, m], op=ADD)
+        nc.vector.tensor_tensor(out=gate[:], in0=gate[:], in1=narrow_sum[:], op=ADD)
+        for m in range(ATOM_TILES):
             nc.vector.tensor_tensor(
                 out=q_new[:, m], in0=narrow_bank[m][:], in1=gate[:, m], op=ADD
             )

@@ -29,7 +29,9 @@ WIDE = 512
 SIZES = [2] * 4 + [4] * 5 + [2] * 2
 UNITS = [(sum(SIZES[:i]), n) for i, n in enumerate(SIZES)]
 LAST = len(UNITS) - 1
-TAIL = (LAST - 2, LAST - 1, LAST)
+TAIL = range(LAST - 3, LAST + 1)
+AHEAD_FROM = LAST - 4
+H_PAIRS_FROM = LAST - 5
 UNIT_OF_PASS = {g: i for i, (first, n) in enumerate(UNITS) for g in range(first, first + n)}
 
 RUN = 16
@@ -45,7 +47,7 @@ def tile_painnmixing_pb_k_kernel(
     with (
         tc.tile_pool(name="keep", bufs=1) as keep,
         tc.tile_pool(name="stage", bufs=2) as stage,
-        tc.tile_pool(name="code_tiles", bufs=4) as code_tiles,
+        tc.tile_pool(name="code_tiles", bufs=5) as code_tiles,
         tc.psum_pool(name="sum_banks", bufs=1) as sum_banks,
         tc.psum_pool(name="flip_banks", bufs=4) as flip_banks,
         tc.manual_schedule(),
@@ -129,14 +131,17 @@ def tile_painnmixing_pb_k_kernel(
 
         def load_rest():
             rows = 0
+            next_h = 4
             for i in range(2, LAST + 1):
                 load_words(i)
                 load_scale_rows(1, rows, 2)
-                if i + 2 <= LAST:
-                    load_h(i + 2)
-                    load_scale_rows(1, rows + 2, 2)
+                for j in range(2 if i >= H_PAIRS_FROM else 1):
+                    if next_h <= LAST:
+                        load_h(next_h)
+                        next_h += 1
+                load_scale_rows(1, rows + 2, 2)
                 rows += 4
-                if i == LAST - 2:
+                if i == LAST:
                     load_factors()
 
         def spread_bias():
@@ -290,7 +295,7 @@ def tile_painnmixing_pb_k_kernel(
         prepare(0)
         for i in range(LAST):
             keep_waiting()
-            prepare(LAST if i + 2 >= LAST else i + 1)
+            prepare(i + 2 if i >= AHEAD_FROM else i + 1)
             if i not in TAIL:
                 for m in range(ATOM_TILES):
                     multiply_wide(passes_of([i]), m)
@@ -305,12 +310,9 @@ def tile_painnmixing_pb_k_kernel(
         out_mu = out_1.rearrange("(p m) c f -> p m (c f)", p=P)
         out_q = out_0.rearrange("(p m) o f -> p m (o f)", p=P)
         for m in range(ATOM_TILES):
-            multiply_wide(passes_of(TAIL[:1]), m)
-        for m in range(ATOM_TILES):
-            multiply_wide(passes_of(TAIL[1:]), m)
+            multiply_wide(passes_of(TAIL), m)
         for m in range(ATOM_TILES):
             multiply_narrow(passes_of(TAIL), m)
-        nc.vector.tensor_tensor(out=narrow_sum[:], in0=narrow_sum[:], in1=q_sb[:], op=ADD)
         for m in range(ATOM_TILES):
             nc.vector.tensor_tensor(
                 out=factors[:, m], in0=wide_sum[m][:], in1=bias[:, F:], op=ADD
@@ -321,14 +323,20 @@ def tile_painnmixing_pb_k_kernel(
                 in1=factors[:, m, :F].unsqueeze(1).to_broadcast([P, AXES, F]),
                 op=MULT,
             )
-        nc.vector.tensor_tensor(out=gate[:], in0=mu_vw_sb[:], in1=factors[:, :, F:], op=MULT)
-        for m in range(ATOM_TILES):
-            adder = nc.vector if m else nc.gpsimd
-            adder.tensor_tensor(out=mu_new[:, m], in0=mu_new[:, m], in1=mu_sb[:, m], op=ADD)
+            nc.vector.tensor_tensor(
+                out=gate[:, m], in0=mu_vw_sb[:, m], in1=factors[:, m, F:], op=MULT
+            )
+            nc.vector.tensor_tensor(out=mu_new[:, m], in0=mu_new[:, m], in1=mu_sb[:, m], op=ADD)
             nc.sync.dma_start(
                 out=out_mu[:, m], in_=mu_new[:, m].rearrange("p c f -> p (c f)")
             )
-        nc.vector.tensor_tensor(out=gate[:], in0=gate[:], in1=narrow_sum[:], op=ADD)
+            if m == 0:
+                nc.vector.tensor_tensor(
+                    out=narrow_sum[:], in0=narrow_sum[:], in1=q_sb[:], op=ADD
+                )
+            nc.vector.tensor_tensor(
+                out=gate[:, m], in0=gate[:, m], in1=narrow_sum[:, m], op=ADD
+            )
         for m in range(ATOM_TILES):
             nc.vector.tensor_tensor(
                 out=q_new[:, m], in0=narrow_bank[m][:], in1=gate[:, m], op=ADD

import concourse.mybir as mybir
from concourse.masks import make_identity

F32 = mybir.dt.float32
BF16 = mybir.dt.bfloat16
I32 = mybir.dt.int32
U32 = mybir.dt.uint32
U8 = mybir.dt.uint8
FP8X4 = mybir.dt.float8_e4m3fn_x4
FP4X4 = mybir.dt.float4_e2m1fn_x4
MULT = mybir.AluOpType.mult
ADD = mybir.AluOpType.add

P = 128
ATOMS = 256
ATOM_TILES = ATOMS // P
K = 16384
PACK = 4
K_PASS = P * PACK
PASSES = K // K_PASS
PAIRS = PACK // 2
F = 256
AXES = 3
COLS = 3 * F

NARROW = 128
WIDE = 512

SIZES = [2] * 4 + [4] * 5 + [2] * 2
UNITS = [(sum(SIZES[:i]), n) for i, n in enumerate(SIZES)]
LAST = len(UNITS) - 1
TAIL = range(LAST - 3, LAST + 1)
AHEAD_FROM = LAST - 4
H_PAIRS_FROM = LAST - 5
UNIT_OF_PASS = {g: i for i, (first, n) in enumerate(UNITS) for g in range(first, first + n)}

RUN = 16
RUNS = PASSES // RUN

FLOPS = 2 * ATOMS * K * COLS


def tile_painnmixing_pb_k_kernel(
    tc, h, mu_W, mu_VW, q, mu, W2_words, W2_scales, b2, out_0, out_1
):
    nc = tc.nc
    with (
        tc.tile_pool(name="keep", bufs=1) as keep,
        tc.tile_pool(name="stage", bufs=2) as stage,
        tc.tile_pool(name="code_tiles", bufs=5) as code_tiles,
        tc.psum_pool(name="sum_banks", bufs=1) as sum_banks,
        tc.psum_pool(name="flip_banks", bufs=4) as flip_banks,
        tc.manual_schedule(),
    ):
        h_sb = [
            keep.tile([P, ATOM_TILES, n * K_PASS], BF16, name="h_%d" % g) for g, n in UNITS
        ]
        w_words = [
            keep.tile([P, n, 2 * COLS], U8, align_bytes=64, name="w_words_%d" % g)
            for g, n in UNITS
        ]
        w_scales = [
            keep.tile([P, RUN, COLS], U8, align_bytes=64, name="w_scales_%d" % i)
            for i in range(RUNS)
        ]
        identity = keep.tile([P, P], F32)
        ones = keep.tile([P, P], BF16)
        bias_rows = keep.tile([P, COLS], BF16)
        bias = keep.tile([P, COLS], F32)
        mu_w_sb = keep.tile([P, ATOM_TILES, AXES, F], BF16)
        mu_sb = keep.tile([P, ATOM_TILES, AXES, F], BF16)
        mu_vw_sb = keep.tile([P, ATOM_TILES, F], BF16)
        q_sb = keep.tile([P, ATOM_TILES, F], BF16)
        factors = keep.tile([P, ATOM_TILES, WIDE], F32)
        narrow_sum = keep.tile([P, ATOM_TILES, F], F32)
        mu_new = keep.tile([P, ATOM_TILES, AXES, F], F32)
        q_new = keep.tile([P, ATOM_TILES, F], F32)
        gate = keep.tile([P, ATOM_TILES, F], F32)

        half = RUN // 2
        nc.vector.memset(w_scales[0][:, :half, :].bitcast(I32), 0)
        nc.gpsimd.memset(w_scales[0][:, half:, :].bitcast(I32), 0)
        make_identity(nc, identity[:])
        nc.vector.memset(bias_rows[:], 0.0)
        nc.vector.memset(ones[:], 1.0)

        nc.scalar.dma_start(out=bias_rows[0:1, :], in_=b2.unsqueeze(0))

        words_dram = W2_words.bitcast(I32)
        scales_dram = W2_scales.bitcast(I32)
        h_rows = h.rearrange("(p m) o k -> p m (o k)", p=P)

        def load_h(i):
            g, n = UNITS[i]
            nc.sync.dma_start(out=h_sb[i][:], in_=h_rows[:, :, g * K_PASS : (g + n) * K_PASS])

        def load_words(i):
            g, n = UNITS[i]
            nc.sync.dma_start(
                out=w_words[i][:].bitcast(I32),
                in_=words_dram[g : g + n].rearrange("g p n -> p g n"),
            )

        def load_scale_rows(run, first, count):
            gs = slice(run * RUN, (run + 1) * RUN)
            for i in range(first, min(first + count, 16)):
                quadrant, r = (0, 2, 1, 3)[i % 4], i // 4
                part, row = 32 * quadrant + r, 4 * quadrant + r
                nc.sync.dma_start(
                    out=w_scales[run][part : part + 1].bitcast(I32),
                    in_=scales_dram[gs, row : row + 1, :].rearrange("g s n -> s g n"),
                )

        def load_factors():
            nc.sync.dma_start(out=mu_w_sb[:], in_=mu_W.rearrange("(p m) c f -> p m c f", p=P))
            nc.sync.dma_start(out=mu_sb[:], in_=mu.rearrange("(p m) c f -> p m c f", p=P))
            nc.sync.dma_start(
                out=mu_vw_sb[:], in_=mu_VW.rearrange("(p m) o f -> p m (o f)", p=P)
            )
            nc.sync.dma_start(out=q_sb[:], in_=q.rearrange("(p m) o f -> p m (o f)", p=P))

        load_h(0)
        load_scale_rows(0, 0, 5)
        load_h(1)
        load_scale_rows(0, 5, 5)
        load_words(0)
        load_scale_rows(0, 10, 6)
        load_h(2)
        load_words(1)
        load_h(3)

        def load_rest():
            rows = 0
            next_h = 4
            for i in range(2, LAST + 1):
                load_words(i)
                load_scale_rows(1, rows, 2)
                for j in range(2 if i >= H_PAIRS_FROM else 1):
                    if next_h <= LAST:
                        load_h(next_h)
                        next_h += 1
                load_scale_rows(1, rows + 2, 2)
                rows += 4
                if i == LAST:
                    load_factors()

        def spread_bias():
            for first, last in ((0, F), (F, COLS)):
                bank = flip_banks.tile([P, last - first], F32, tag="flip", name="bias_%d" % first)
                nc.tensor.matmul(
                    out=bank[:], lhsT=ones[:], rhs=bias_rows[:, first:last], start=True, stop=True
                )
                nc.scalar.copy(out=bias[:, first:last], in_=bank[:])

        sorted_words = {}
        grouped = {}
        flipped = {}
        h_codes = {}
        h_scales = {}
        wide_sum = [
            sum_banks.tile([P, WIDE], F32, name="wide_sum_%d" % m) for m in range(ATOM_TILES)
        ]
        narrow_bank = [
            sum_banks.tile([P, F], F32, name="narrow_sum_%d" % m) for m in range(ATOM_TILES)
        ]

        def sort_words(i):
            g, n = UNITS[i]
            words = stage.tile(
                [P, ATOM_TILES * n, PAIRS, P], F32, tag="sorted", name="sorted_%d" % i, bufs=3
            )
            nc.vector.tensor_copy(
                out=words[:],
                in_=h_sb[i][:]
                .rearrange("p m k -> p (m k)")
                .bitcast(F32)
                .rearrange("p (n w u) -> p n u w", w=P, u=PAIRS),
            )
            for j in range(n):
                for m in range(ATOM_TILES):
                    sorted_words[(g + j, m)] = words[:, m * n + j]

        def flip(i):
            first, n = UNITS[i]
            for g in range(first, first + n):
                flipped[g] = flip_banks.tile(
                    [P, PAIRS, ATOMS], F32, tag="flip", name="flipped_%d" % g
                )
                for u in range(PAIRS):
                    for m in range(ATOM_TILES):
                        nc.tensor.transpose(
                            flipped[g][:, u, m * P : (m + 1) * P],
                            sorted_words[(g, m)][:, u, :],
                            identity[:],
                        )

        def group(i):
            g, n = UNITS[i]
            grouped[i] = stage.tile(
                [P, n, ATOMS, PACK], BF16, align_bytes=64, tag="grouped", name="grouped_%d" % i
            )
            words = grouped[i][:].bitcast(F32)
            for j in range(n):
                nc.scalar.copy(out=words[:, j], in_=flipped[g + j][:].rearrange("p u a -> p a u"))

        def quantize(i):
            g, n = UNITS[i]
            codes = code_tiles.tile(
                [P, n, ATOMS], U32, align_bytes=64, tag="codes", name="codes_%d" % i
            )
            scales = code_tiles.tile(
                [P, n, ATOMS], U8, align_bytes=64, tag="scales", name="scales_%d" % i
            )
            nc.vector.quantize_mx(
                out=codes[:].rearrange("p g a -> p (g a)").bitcast(FP8X4),
                scales=scales[:].rearrange("p g a -> p (g a)"),
                in_=grouped[i][:].rearrange("p g a t -> p (g a t)"),
            )
            for j in range(n):
                h_codes[g + j] = codes[:, j]
                h_scales[g + j] = scales[:, j]

        def mx_pass(g, m, out, first, width, start, stop):
            atoms = slice(m * P, (m + 1) * P)
            unit = UNIT_OF_PASS[g]
            nc.tensor.matmul_mx(
                out=out,
                lhsT=h_codes[g][:, atoms].bitcast(FP8X4),
                lhsT_scale=h_scales[g][:, atoms],
                rhs=w_words[unit][
                    :, g - UNITS[unit][0], 2 * first : 2 * (first + width)
                ].bitcast(FP4X4),
                rhs_scale=w_scales[g // RUN][:, g % RUN, first : first + width],
                start=start,
                stop=stop,
            )

        def multiply_wide(passes, m):
            for g in passes:
                mx_pass(g, m, wide_sum[m][:], F, WIDE, g == 0, g == PASSES - 1)

        def multiply_narrow(passes, m):
            for first in range(0, F, NARROW):
                for g in passes:
                    mx_pass(
                        g, m, narrow_bank[m][:, first : first + NARROW], first, NARROW,
                        g == passes[0], g == passes[-1],
                    )

        def keep_narrow(first, m):
            nc.vector.tensor_tensor(
                out=narrow_sum[:, m],
                in0=narrow_bank[m][:],
                in1=bias[:, :F] if first else narrow_sum[:, m],
                op=ADD,
            )

        def passes_of(units):
            return [g for i in units for g in range(UNITS[i][0], UNITS[i][0] + UNITS[i][1])]

        narrow_units = {}
        waiting = []
        for i in range(LAST + 1):
            waiting.append(i)
            if len(passes_of(waiting)) >= 4:
                narrow_units[i] = waiting
                waiting = []
        sorted_to = [0]
        ready = [0]
        to_keep = []

        def sort_to(i):
            while sorted_to[0] <= min(i, LAST):
                sort_words(sorted_to[0])
                sorted_to[0] += 1

        def prepare(last_unit):
            while ready[0] <= min(last_unit, LAST):
                i = ready[0]
                sort_to(LAST if i >= LAST - 2 else i + 1)
                flip(i)
                group(i)
                quantize(i)
                ready[0] += 1

        def keep_waiting():
            for i in to_keep:
                for m in range(ATOM_TILES):
                    keep_narrow(narrow_units[i][0] == 0, m)
            to_keep.clear()

        sort_to(1)
        nc.vector.memset(w_scales[1][:].bitcast(I32), 0)
        load_rest()
        prepare(0)
        for i in range(LAST):
            keep_waiting()
            prepare(i + 2 if i >= AHEAD_FROM else i + 1)
            if i not in TAIL:
                for m in range(ATOM_TILES):
                    multiply_wide(passes_of([i]), m)
                if i in narrow_units:
                    for m in range(ATOM_TILES):
                        multiply_narrow(passes_of(narrow_units[i]), m)
                    to_keep.append(i)
                if i == 0:
                    spread_bias()
        keep_waiting()

        out_mu = out_1.rearrange("(p m) c f -> p m (c f)", p=P)
        out_q = out_0.rearrange("(p m) o f -> p m (o f)", p=P)
        for m in range(ATOM_TILES):
            multiply_wide(passes_of(TAIL), m)
        for m in range(ATOM_TILES):
            multiply_narrow(passes_of(TAIL), m)
        for m in range(ATOM_TILES):
            nc.vector.tensor_tensor(
                out=factors[:, m], in0=wide_sum[m][:], in1=bias[:, F:], op=ADD
            )
            nc.vector.tensor_tensor(
                out=mu_new[:, m],
                in0=mu_w_sb[:, m],
                in1=factors[:, m, :F].unsqueeze(1).to_broadcast([P, AXES, F]),
                op=MULT,
            )
            nc.vector.tensor_tensor(
                out=gate[:, m], in0=mu_vw_sb[:, m], in1=factors[:, m, F:], op=MULT
            )
            nc.vector.tensor_tensor(out=mu_new[:, m], in0=mu_new[:, m], in1=mu_sb[:, m], op=ADD)
            nc.sync.dma_start(
                out=out_mu[:, m], in_=mu_new[:, m].rearrange("p c f -> p (c f)")
            )
            if m == 0:
                nc.vector.tensor_tensor(
                    out=narrow_sum[:], in0=narrow_sum[:], in1=q_sb[:], op=ADD
                )
            nc.vector.tensor_tensor(
                out=gate[:, m], in0=gate[:, m], in1=narrow_sum[:, m], op=ADD
            )
        for m in range(ATOM_TILES):
            nc.vector.tensor_tensor(
                out=q_new[:, m], in0=narrow_bank[m][:], in1=gate[:, m], op=ADD
            )
            nc.sync.dma_start(out=out_q[:, m], in_=q_new[:, m])
